import numpy as np
import ml_dtypes


def mxq(x, axis, fmt="e4m3"):
    dtype, down = {"e4m3": (ml_dtypes.float8_e4m3fn, 7), "e5m2": (ml_dtypes.float8_e5m2, 14)}[fmt]
    v = np.moveaxis(np.asarray(x, np.float32).astype(ml_dtypes.bfloat16).astype(np.float64), axis, -1)
    blocks = v.reshape(v.shape[:-1] + (-1, 32))
    amax = np.abs(blocks).max(-1, keepdims=True)
    byte = np.maximum(np.where(amax > 0, np.frexp(amax)[1] - 1 + 127, 0) - down, 1)
    scale = np.exp2(byte - 127.0)
    codes = (blocks / scale).astype(np.float32).astype(dtype).astype(np.float64)
    return np.moveaxis((codes * scale).reshape(v.shape), -1, axis)


WIDE = False


def mx_kscale(k):
    if not WIDE:
        return np.ones(k)
    levels = np.array([10, -10, 5, -5, 0])
    a = np.random.permutation(np.resize(levels, k // 512 * 4)).reshape(k // 512, 4)
    idx = np.arange(k)
    return np.exp2(a[idx // 512, idx % 128 // 32])


BF16 = ml_dtypes.bfloat16


def bf(x):
    return np.asarray(x, np.float32).astype(BF16)


def f64(x):
    return np.asarray(x).astype(np.float64)


N, H0C, W0C, H1C, W1C, C = 1, 64, 64, 32, 32, 512
L, S = H0C * W0C, H1C * W1C
P = max(L, S)
THR = 0.2
BORDER = 2
TEMP_INIT = 10.0


def softmax(v, axis):
    e = np.exp(v - v.max(axis=axis, keepdims=True))
    return e / e.sum(axis=axis, keepdims=True)


def border_mask():
    def ok(n):
        a = np.arange(n)
        return (a >= BORDER) & (a < n - BORDER)
    m = (ok(H0C)[:, None, None, None] & ok(W0C)[None, :, None, None]
         & ok(H1C)[None, None, :, None] & ok(W1C)[None, None, None, :])
    return m.reshape(L, S)


def setup_inputs():
    s = mx_kscale(C)
    g = np.random.standard_normal((N, P, C))
    i0 = np.random.randint(0, P, (N, L))
    i1 = np.random.randint(0, P, (N, S))
    n = np.arange(N)[:, None]
    c0 = np.sqrt(0.9) * g[n, i0] + np.sqrt(0.1) * np.random.standard_normal((N, L, C))
    c1 = np.sqrt(0.9) * g[n, i1] + np.sqrt(0.1) * np.random.standard_normal((N, S, C))
    return {"feat_c0": bf(c0 * s), "feat_c1": bf(c1 / s),
            "temperature": bf(TEMP_INIT * (1.0 + 0.03 * np.random.standard_normal(1)))}


def reference(feat_c0, feat_c1, temperature):
    inv_sqrt_c = 1.0 / float(C) ** 0.5
    f0 = f64(feat_c0) * inv_sqrt_c
    f1 = f64(feat_c1) * inv_sqrt_c
    sim = (mxq(f0, 2, "e4m3") @ mxq(f1, 2, "e4m3").transpose(0, 2, 1)) * f64(temperature)
    conf = softmax(sim, 1) * softmax(sim, 2)
    mask = (conf > THR) & border_mask()[None]
    mutual = (mask
              & (conf == conf.max(axis=2, keepdims=True))
              & (conf == conf.max(axis=1, keepdims=True)))
    mconf = np.where(mutual, conf, 0.0)
    return conf, mconf

@@ -1,0 +1,285 @@
+import concourse.mybir as mybir
+from concourse.masks import make_identity
+
+F32 = mybir.dt.float32
+BF16 = mybir.dt.bfloat16
+U32 = mybir.dt.uint32
+U8 = mybir.dt.uint8
+FP8X4 = mybir.dt.float8_e4m3fn_x4
+ALU = mybir.AluOpType
+ACT = mybir.ActivationFunctionType
+AX = mybir.AxisListType
+
+P = 128
+L = 4096
+S = 1024
+C = 512
+LT = L // P
+ST = S // P
+NB = 512
+LC = L // NB
+THR = 0.2
+INV_SQRT_C = 1.0 / float(C) ** 0.5
+NEVER = 2.0
+S_LO = 64
+S_HI = 960
+N_MC = 4
+
+FLOPS = 2 * L * S * C
+
+
+def tile_coarsematching_t_kernel(tc, feat_c0, feat_c1, temperature, out_0, out_1):
+    nc = tc.nc
+    f0 = feat_c0.flatten_outer_dims()
+    f1 = feat_c1.flatten_outer_dims()
+    o0 = out_0.flatten_outer_dims()
+    o1 = out_1.flatten_outer_dims()
+
+    with tc.tile_pool(name="keep", bufs=1) as keep, tc.tile_pool(name="junk", bufs=2) as junk, tc.psum_pool(
+        name="psm", bufs=5
+    ) as psm, tc.psum_pool(name="pst", bufs=3) as pst:
+        ident = keep.tile([P, P], F32, name="ident")
+        make_identity(nc, ident[:])
+
+        t_bf = keep.tile([P, 1], BF16, name="t_bf")
+        nc.sync.dma_start(out=t_bf[:], in_=temperature.partition_broadcast(P))
+        t_pos = keep.tile([P, 1], F32, name="t_pos")
+        t_neg = keep.tile([P, 1], F32, name="t_neg")
+        t_two = keep.tile([P, 1], F32, name="t_two")
+        nc.vector.tensor_copy(out=t_pos[:], in_=t_bf[:])
+        nc.vector.tensor_scalar(out=t_neg[:], in0=t_bf[:], scalar1=-1.0, scalar2=None, op0=ALU.mult)
+        nc.vector.tensor_scalar(out=t_two[:], in0=t_bf[:], scalar1=2.0, scalar2=None, op0=ALU.mult)
+
+        edge = keep.tile([P, 4], F32, name="edge")
+        id64 = ident[:].rearrange("p (a b) -> p a b", b=64)
+        id32 = ident[:].rearrange("p (a b) -> p a b", b=32)
+        nc.vector.tensor_reduce(out=edge[:, 0:1], in_=id64[:, :, 0:2], axis=AX.XY, op=ALU.add)
+        nc.vector.tensor_reduce(out=edge[:, 1:2], in_=id64[:, :, 62:64], axis=AX.XY, op=ALU.add)
+        nc.vector.tensor_reduce(out=edge[:, 2:3], in_=id32[:, :, 0:2], axis=AX.XY, op=ALU.add)
+        nc.vector.tensor_reduce(out=edge[:, 3:4], in_=id32[:, :, 30:32], axis=AX.XY, op=ALU.add)
+        row_edge = keep.tile([P, 1], F32, name="row_edge")
+        col_edge = keep.tile([P, 1], F32, name="col_edge")
+        nc.vector.tensor_tensor(out=row_edge[:], in0=edge[:, 0:1], in1=edge[:, 1:2], op=ALU.add)
+        nc.vector.tensor_tensor(out=col_edge[:], in0=edge[:, 2:3], in1=edge[:, 3:4], op=ALU.add)
+        nc.vector.tensor_scalar(out=row_edge[:], in0=row_edge[:], scalar1=NEVER, scalar2=None, op0=ALU.mult)
+        nc.vector.tensor_scalar(out=col_edge[:], in0=col_edge[:], scalar1=NEVER, scalar2=None, op0=ALU.mult)
+
+        c0 = keep.tile([P, L], U32, name="c0", align_bytes=64)
+        s0 = keep.tile([P, L], U8, name="s0", align_bytes=64)
+        c1 = keep.tile([P, S], U32, name="c1", align_bytes=64)
+        s1 = keep.tile([P, S], U8, name="s1", align_bytes=64)
+
+        nm = keep.tile([P, 128], F32, name="nm")
+        sg = keep.tile([P, 128], F32, name="sg")
+
+        def mx(bank, codes_a, scales_a, a_lo, codes_b, scales_b, b_lo):
+            nc.tensor.matmul_mx(
+                out=bank,
+                lhsT=codes_a[:, a_lo : a_lo + P].bitcast(FP8X4),
+                lhsT_scale=scales_a[:, a_lo : a_lo + P],
+                rhs=codes_b[:, b_lo : b_lo + NB].bitcast(FP8X4),
+                rhs_scale=scales_b[:, b_lo : b_lo + NB],
+                start=True,
+                stop=True,
+            )
+
+        def stat_unit(col, codes_a, scales_a, a_lo, codes_b, scales_b, b_lo):
+            bank = psm.tile([P, NB], F32, name="bank", tag="mx")
+            mx(bank[:], codes_a, scales_a, a_lo, codes_b, scales_b, b_lo)
+            jv = junk.tile([P, NB], BF16, name="jv", tag="jv")
+            nc.vector.tensor_scalar(
+                out=jv[:],
+                in0=bank[:],
+                scalar1=t_neg[:, 0:1],
+                scalar2=None,
+                op0=ALU.mult,
+                op1=ALU.min,
+                accum_out=nm[:, col : col + 1],
+            )
+            js = junk.tile([P, NB], BF16, name="js", tag="js")
+            nc.scalar.activation(
+                out=js[:],
+                in_=bank[:],
+                func=ACT.Exp,
+                bias=nm[:, col : col + 1],
+                scale=t_pos[:, 0:1],
+                accum_out=sg[:, col : col + 1],
+            )
+
+        with tc.tile_pool(name="head", bufs=3) as head:
+
+            def prepare(raw, codes, scales, lo):
+                grouped = head.tile([P, NB, 4], BF16, name="grouped", tag="grouped", align_bytes=64)
+                for half in range(2):
+                    bank = pst.tile([P, 2, 256], F32, name="tbank", tag="tr")
+                    for i in range(2):
+                        words = raw[:, 2 * half + i, :].bitcast(F32)
+                        for u in range(2):
+                            nc.tensor.transpose(
+                                bank[:, u, P * i : P * (i + 1)], words[:, P * u : P * (u + 1)], ident[:]
+                            )
+                    src = bank[:].bitcast(BF16).rearrange("p u (l e) -> p l u e", e=2)
+                    dst = grouped[:, 256 * half : 256 * (half + 1), :].rearrange("p l (u e) -> p l u e", e=2)
+                    if half == 0:
+                        nc.vector.tensor_scalar(out=dst, in0=src, scalar1=INV_SQRT_C, scalar2=None, op0=ALU.mult)
+                    else:
+                        nc.scalar.activation(out=dst, in_=src, func=ACT.Copy, scale=INV_SQRT_C)
+                nc.vector.quantize_mx(
+                    out=codes[:, lo : lo + NB].bitcast(FP8X4),
+                    scales=scales[:, lo : lo + NB],
+                    in_=grouped[:].rearrange("p l j -> p (l j)"),
+                )
+
+            raw1 = head.tile([P, ST, C], BF16, name="raw1", tag="raw1", bufs=1)
+            nc.sync.dma_start(out=raw1[:], in_=f1.rearrange("(t p) k -> p t k", p=P))
+            raws = []
+            for c in range(LC):
+                raw0 = head.tile([P, 4, C], BF16, name="raw0", tag="raw0")
+                nc.sync.dma_start(out=raw0[:], in_=f0[c * NB : (c + 1) * NB, :].rearrange("(t p) k -> p t k", p=P))
+                raws.append(raw0)
+                if c == 0:
+                    prepare(raw1[:, 0:4, :], c1, s1, 0)
+                    prepare(raw1[:, 4:8, :], c1, s1, NB)
+                prepare(raw0, c0, s0, c * NB)
+                for j in range(4):
+                    t = 4 * c + j
+                    for h in range(2):
+                        stat_unit(2 * t + h, c0, s0, t * P, c1, s1, h * NB)
+                for st in range(ST):
+                    stat_unit(64 + ST * st + c, c1, s1, st * P, c0, s0, c * NB)
+
+        nmx = keep.tile([P, 40], F32, name="nmx")
+        dd = keep.tile([P, 128], F32, name="dd")
+        tot = keep.tile([P, 40], F32, name="tot")
+        ab = keep.tile([P, 40], F32, name="ab")
+        nm_r = nm[:, 0:64].rearrange("p (t h) -> p t h", h=2)
+        nm_c = nm[:, 64:128].rearrange("p (t h) -> p t h", h=LC)
+        dd_r = dd[:, 0:64].rearrange("p (t h) -> p t h", h=2)
+        dd_c = dd[:, 64:128].rearrange("p (t h) -> p t h", h=LC)
+        nc.vector.tensor_reduce(out=nmx[:, 0:32], in_=nm_r, axis=AX.X, op=ALU.min)
+        nc.vector.tensor_reduce(out=nmx[:, 32:40], in_=nm_c, axis=AX.X, op=ALU.min)
+        nc.vector.tensor_tensor(
+            out=dd_r, in0=nmx[:, 0:32].unsqueeze(2).to_broadcast([P, LT, 2]), in1=nm_r, op=ALU.subtract
+        )
+        nc.vector.tensor_tensor(
+            out=dd_c, in0=nmx[:, 32:40].unsqueeze(2).to_broadcast([P, ST, LC]), in1=nm_c, op=ALU.subtract
+        )
+        nc.scalar.activation(out=dd[:], in_=dd[:], func=ACT.Exp)
+        nc.vector.tensor_tensor(out=dd[:], in0=dd[:], in1=sg[:], op=ALU.mult)
+        nc.vector.tensor_reduce(out=tot[:, 0:32], in_=dd_r, axis=AX.X, op=ALU.add)
+        nc.vector.tensor_reduce(out=tot[:, 32:40], in_=dd_c, axis=AX.X, op=ALU.add)
+        nc.scalar.activation(out=tot[:], in_=tot[:], func=ACT.Ln)
+        nc.vector.tensor_tensor(out=ab[:], in0=nmx[:], in1=tot[:], op=ALU.subtract)
+
+        with tc.tile_pool(name="main", bufs=1) as main:
+            conf = main.tile([P, LT, S], F32, name="conf")
+            best = main.tile([P, S], F32, name="best")
+            mcs = [main.tile([P, S], F32, name="mc%d" % i) for i in range(N_MC)]
+            for i in range(N_MC):
+                nc.gpsimd.memset(mcs[i][:], 0.0)
+            nc.gpsimd.memset(best[:, 0:S_LO], 0.0)
+            nc.gpsimd.memset(best[:, S_HI:S], 0.0)
+            nc.sync.dma_start(out=o1[0:P, :], in_=mcs[0][:])
+            nc.sync.dma_start(out=o1[L - P : L, :], in_=mcs[1][:])
+            rt2 = main.tile([P, 2 * LT], F32, name="rt2")
+
+            def columns(c, w1, st):
+                bank = psm.tile([P, NB], F32, name="bank", tag="mx")
+                mx(bank[:], c1, s1, st * P, c0, s0, c * NB)
+                nc.scalar.activation(
+                    out=w1[:, st, :],
+                    in_=bank[:],
+                    func=ACT.Identity,
+                    bias=ab[:, 32 + st : 33 + st],
+                    scale=t_two[:, 0:1],
+                )
+
+            def rows(c, w1, j):
+                t = 4 * c + j
+                for h in range(2):
+                    tb = pst.tile([P, NB], F32, name="tb", tag="tr")
+                    for q in range(4):
+                        nc.tensor.transpose(
+                            tb[:, q * P : (q + 1) * P], w1[:, 4 * h + q, j * P : (j + 1) * P], ident[:]
+                        )
+                    nc.vector.tensor_scalar(
+                        out=conf[:, t, h * NB : (h + 1) * NB],
+                        in0=tb[:],
+                        scalar1=ab[:, t : t + 1],
+                        scalar2=None,
+                        op0=ALU.add,
+                        op1=ALU.max,
+                        accum_out=rt2[:, 2 * t + h : 2 * t + h + 1],
+                    )
+                nc.scalar.activation(out=conf[:, t, :], in_=conf[:, t, :], func=ACT.Exp)
+                nc.sync.dma_start(out=o0[t * P : (t + 1) * P, :], in_=conf[:, t, :])
+                if t == 1:
+                    nc.vector.tensor_tensor(
+                        out=best[:, S_LO:S_HI], in0=conf[:, 0, S_LO:S_HI], in1=conf[:, 1, S_LO:S_HI], op=ALU.max
+                    )
+                elif t > 1:
+                    nc.vector.tensor_tensor(
+                        out=best[:, S_LO:S_HI], in0=best[:, S_LO:S_HI], in1=conf[:, t, S_LO:S_HI], op=ALU.max
+                    )
+
+            w1_now = main.tile([P, ST, NB], F32, name="w1", tag="w1", bufs=2)
+            for st in range(ST):
+                columns(0, w1_now, st)
+            for c in range(LC):
+                w1_next = None
+                if c + 1 < LC:
+                    w1_next = main.tile([P, ST, NB], F32, name="w1", tag="w1", bufs=2)
+                for j in range(4):
+                    if c + 1 < LC:
+                        columns(c + 1, w1_next, 2 * j)
+                        columns(c + 1, w1_next, 2 * j + 1)
+                    rows(c, w1_now, j)
+                w1_now = w1_next
+
+            rmax = main.tile([P, LT], F32, name="rmax")
+            rgate = main.tile([P, LT], F32, name="rgate")
+            nc.vector.tensor_reduce(out=rmax[:], in_=rt2[:].rearrange("p (t h) -> p t h", h=2), axis=AX.X, op=ALU.max)
+            nc.scalar.activation(out=rmax[:], in_=rmax[:], func=ACT.Exp)
+            nc.vector.tensor_scalar(out=rgate[:], in0=rmax[:], scalar1=THR, scalar2=NEVER, op0=ALU.is_le, op1=ALU.mult)
+            nc.vector.tensor_tensor(out=rgate[:], in0=rgate[:], in1=rmax[:], op=ALU.max)
+            nc.vector.tensor_scalar(out=rgate[:], in0=rgate[:], scalar1=row_edge[:, 0:1], scalar2=None, op0=ALU.max)
+
+            cmax = main.tile([P, ST], F32, name="cmax")
+            for h in range(2):
+                tm = pst.tile([P, 4, P], F32, name="tm", tag="tr")
+                for q in range(4):
+                    st = 4 * h + q
+                    nc.tensor.transpose(tm[:, q, :], best[:, st * P : (st + 1) * P], ident[:])
+                nc.vector.tensor_reduce(out=cmax[:, 4 * h : 4 * h + 4], in_=tm[:], axis=AX.X, op=ALU.max)
+            nc.vector.tensor_scalar(out=cmax[:], in0=cmax[:], scalar1=col_edge[:, 0:1], scalar2=None, op0=ALU.max)
+            spread = main.tile([P, ST, P], F32, name="spread")
+            nc.vector.tensor_copy(out=spread[:], in_=cmax[:].unsqueeze(2).to_broadcast([P, ST, P]))
+            cbs = []
+            for h in range(2):
+                cb = pst.tile([P, NB], F32, name="cb", tag="tr")
+                for q in range(4):
+                    nc.tensor.transpose(cb[:, q * P : (q + 1) * P], spread[:, 4 * h + q, :], ident[:])
+                cbs.append(cb)
+
+            half = (S_HI - S_LO) // 2
+            for t in range(1, LT - 1):
+                mask = main.tile([P, S_HI - S_LO], BF16, name="mask", tag="mask", bufs=3)
+                nc.vector.scalar_tensor_tensor(
+                    out=mask[:, 0:half],
+                    in0=cbs[0][:, S_LO:NB],
+                    scalar=rgate[:, t : t + 1],
+                    in1=conf[:, t, S_LO:NB],
+                    op0=ALU.max,
+                    op1=ALU.is_equal,
+                )
+                nc.vector.scalar_tensor_tensor(
+                    out=mask[:, half : 2 * half],
+                    in0=cbs[1][:, 0 : S_HI - NB],
+                    scalar=rgate[:, t : t + 1],
+                    in1=conf[:, t, NB:S_HI],
+                    op0=ALU.max,
+                    op1=ALU.is_equal,
+                )
+                mc = mcs[t % N_MC]
+                nc.scalar.activation(out=mc[:, S_LO:S_HI], in_=mask[:], func=ACT.Copy, scale=rmax[:, t : t + 1])
+                nc.sync.dma_start(out=o1[t * P : (t + 1) * P, :], in_=mc[:])

@@ -23,6 +23,7 @@ INV_SQRT_C = 1.0 / float(C) ** 0.5
 NEVER = 2.0
 S_LO = 64
 S_HI = 960
+S_IN = S_HI - S_LO
 N_MC = 4
 
 FLOPS = 2 * L * S * C
@@ -35,18 +36,16 @@ def tile_coarsematching_t_kernel(tc, feat_c0, feat_c1, temperature, out_0, out_1
     o0 = out_0.flatten_outer_dims()
     o1 = out_1.flatten_outer_dims()
 
-    with tc.tile_pool(name="keep", bufs=1) as keep, tc.tile_pool(name="junk", bufs=2) as junk, tc.psum_pool(
-        name="psm", bufs=5
-    ) as psm, tc.psum_pool(name="pst", bufs=3) as pst:
+    with tc.tile_pool(name="keep", bufs=1) as keep, tc.psum_pool(name="psm", bufs=5) as psm, tc.psum_pool(
+        name="pst", bufs=3
+    ) as pst:
         ident = keep.tile([P, P], F32, name="ident")
         make_identity(nc, ident[:])
 
         t_bf = keep.tile([P, 1], BF16, name="t_bf")
         nc.sync.dma_start(out=t_bf[:], in_=temperature.partition_broadcast(P))
-        t_pos = keep.tile([P, 1], F32, name="t_pos")
         t_neg = keep.tile([P, 1], F32, name="t_neg")
         t_two = keep.tile([P, 1], F32, name="t_two")
-        nc.vector.tensor_copy(out=t_pos[:], in_=t_bf[:])
         nc.vector.tensor_scalar(out=t_neg[:], in0=t_bf[:], scalar1=-1.0, scalar2=None, op0=ALU.mult)
         nc.vector.tensor_scalar(out=t_two[:], in0=t_bf[:], scalar1=2.0, scalar2=None, op0=ALU.mult)
 
@@ -69,8 +68,11 @@ def tile_coarsematching_t_kernel(tc, feat_c0, feat_c1, temperature, out_0, out_1
         c1 = keep.tile([P, S], U32, name="c1", align_bytes=64)
         s1 = keep.tile([P, S], U8, name="s1", align_bytes=64)
 
-        nm = keep.tile([P, 128], F32, name="nm")
-        sg = keep.tile([P, 128], F32, name="sg")
+        NG = LC // 2
+        nm_bank_r = keep.tile([P, 2 * LT], F32, name="nm_bank_r")
+        nm_bank_c = keep.tile([P, NG, ST, 2], F32, name="nm_bank_c")
+        nms = keep.tile([P, LT + NG * ST], F32, name="nms")
+        sums = keep.tile([P, LT + NG * ST], F32, name="sums")
 
         def mx(bank, codes_a, scales_a, a_lo, codes_b, scales_b, b_lo):
             nc.tensor.matmul_mx(
@@ -83,32 +85,33 @@ def tile_coarsematching_t_kernel(tc, feat_c0, feat_c1, temperature, out_0, out_1
                 stop=True,
             )
 
-        def stat_unit(col, codes_a, scales_a, a_lo, codes_b, scales_b, b_lo):
+        def negated(dst, nm_col, codes_a, scales_a, a_lo, codes_b, scales_b, b_lo):
             bank = psm.tile([P, NB], F32, name="bank", tag="mx")
             mx(bank[:], codes_a, scales_a, a_lo, codes_b, scales_b, b_lo)
-            jv = junk.tile([P, NB], BF16, name="jv", tag="jv")
             nc.vector.tensor_scalar(
-                out=jv[:],
+                out=dst,
                 in0=bank[:],
                 scalar1=t_neg[:, 0:1],
                 scalar2=None,
                 op0=ALU.mult,
                 op1=ALU.min,
-                accum_out=nm[:, col : col + 1],
-            )
-            js = junk.tile([P, NB], BF16, name="js", tag="js")
-            nc.scalar.activation(
-                out=js[:],
-                in_=bank[:],
-                func=ACT.Exp,
-                bias=nm[:, col : col + 1],
-                scale=t_pos[:, 0:1],
-                accum_out=sg[:, col : col + 1],
+                accum_out=nm_col,
             )
 
-        with tc.tile_pool(name="head", bufs=3) as head:
+        with tc.tile_pool(name="head", bufs=3) as head, tc.tile_pool(name="stage", bufs=2) as stage:
 
-            def prepare(raw, codes, scales, lo):
+            def exp_sum(src, col):
+                js = stage.tile([P, 2 * NB], BF16, name="js", tag="js")
+                nc.scalar.activation(
+                    out=js[:],
+                    in_=src,
+                    func=ACT.Exp,
+                    bias=nms[:, col : col + 1],
+                    scale=-1.0,
+                    accum_out=sums[:, col : col + 1],
+                )
+
+            def prepare(raw, codes, scales, lo, engines):
                 grouped = head.tile([P, NB, 4], BF16, name="grouped", tag="grouped", align_bytes=64)
                 for half in range(2):
                     bank = pst.tile([P, 2, 256], F32, name="tbank", tag="tr")
@@ -120,7 +123,7 @@ def tile_coarsematching_t_kernel(tc, feat_c0, feat_c1, temperature, out_0, out_1
                             )
                     src = bank[:].bitcast(BF16).rearrange("p u (l e) -> p l u e", e=2)
                     dst = grouped[:, 256 * half : 256 * (half + 1), :].rearrange("p l (u e) -> p l u e", e=2)
-                    if half == 0:
+                    if engines[half] == "v":
                         nc.vector.tensor_scalar(out=dst, in0=src, scalar1=INV_SQRT_C, scalar2=None, op0=ALU.mult)
                     else:
                         nc.scalar.activation(out=dst, in_=src, func=ACT.Copy, scale=INV_SQRT_C)
@@ -130,69 +133,123 @@ def tile_coarsematching_t_kernel(tc, feat_c0, feat_c1, temperature, out_0, out_1
                     in_=grouped[:].rearrange("p l j -> p (l j)"),
                 )
 
-            raw1 = head.tile([P, ST, C], BF16, name="raw1", tag="raw1", bufs=1)
-            nc.sync.dma_start(out=raw1[:], in_=f1.rearrange("(t p) k -> p t k", p=P))
-            raws = []
-            for c in range(LC):
-                raw0 = head.tile([P, 4, C], BF16, name="raw0", tag="raw0")
-                nc.sync.dma_start(out=raw0[:], in_=f0[c * NB : (c + 1) * NB, :].rearrange("(t p) k -> p t k", p=P))
-                raws.append(raw0)
-                if c == 0:
-                    prepare(raw1[:, 0:4, :], c1, s1, 0)
-                    prepare(raw1[:, 4:8, :], c1, s1, NB)
-                prepare(raw0, c0, s0, c * NB)
+            def row_stats(c, per_tile):
+                nxr = stage.tile([P, 4, S], F32, name="nxr", tag="nxr")
                 for j in range(4):
                     t = 4 * c + j
                     for h in range(2):
-                        stat_unit(2 * t + h, c0, s0, t * P, c1, s1, h * NB)
-                for st in range(ST):
-                    stat_unit(64 + ST * st + c, c1, s1, st * P, c0, s0, c * NB)
+                        negated(
+                            nxr[:, j, h * NB : (h + 1) * NB],
+                            nm_bank_r[:, 2 * t + h : 2 * t + h + 1],
+                            c0, s0, t * P, c1, s1, h * NB,
+                        )
+                    if per_tile:
+                        nc.vector.tensor_tensor(
+                            out=nms[:, t : t + 1],
+                            in0=nm_bank_r[:, 2 * t : 2 * t + 1],
+                            in1=nm_bank_r[:, 2 * t + 1 : 2 * t + 2],
+                            op=ALU.min,
+                        )
+                        exp_sum(nxr[:, j, :], t)
+                if not per_tile:
+                    nc.vector.tensor_reduce(
+                        out=nms[:, 4 * c : 4 * c + 4],
+                        in_=nm_bank_r[:, 8 * c : 8 * c + 8].rearrange("p (t h) -> p t h", h=2),
+                        axis=AX.X,
+                        op=ALU.min,
+                    )
+                    for j in range(4):
+                        exp_sum(nxr[:, j, :], 4 * c + j)
 
-        nmx = keep.tile([P, 40], F32, name="nmx")
-        dd = keep.tile([P, 128], F32, name="dd")
-        tot = keep.tile([P, 40], F32, name="tot")
-        ab = keep.tile([P, 40], F32, name="ab")
-        nm_r = nm[:, 0:64].rearrange("p (t h) -> p t h", h=2)
-        nm_c = nm[:, 64:128].rearrange("p (t h) -> p t h", h=LC)
-        dd_r = dd[:, 0:64].rearrange("p (t h) -> p t h", h=2)
-        dd_c = dd[:, 64:128].rearrange("p (t h) -> p t h", h=LC)
-        nc.vector.tensor_reduce(out=nmx[:, 0:32], in_=nm_r, axis=AX.X, op=ALU.min)
-        nc.vector.tensor_reduce(out=nmx[:, 32:40], in_=nm_c, axis=AX.X, op=ALU.min)
+            def col_stats(g):
+                nxc = stage.tile([P, ST, 2 * NB], F32, name="nxc", tag="nxc")
+                for st in range(ST):
+                    for cc in range(2):
+                        negated(
+                            nxc[:, st, cc * NB : (cc + 1) * NB],
+                            nm_bank_c[:, g, st, cc : cc + 1],
+                            c1, s1, st * P, c0, s0, (2 * g + cc) * NB,
+                        )
+                lo = LT + g * ST
+                nc.vector.tensor_reduce(out=nms[:, lo : lo + ST], in_=nm_bank_c[:, g, :, :], axis=AX.X, op=ALU.min)
+                for st in range(ST):
+                    exp_sum(nxc[:, st, :], lo + st)
+
+            raw1 = head.tile([P, ST, C], BF16, name="raw1", tag="raw1", bufs=1)
+            nc.sync.dma_start(out=raw1[:], in_=f1.rearrange("(t p) k -> p t k", p=P))
+            for g in range(NG):
+                for cc in range(2):
+                    c = 2 * g + cc
+                    raw0 = head.tile([P, 4, C], BF16, name="raw0", tag="raw0")
+                    nc.sync.dma_start(
+                        out=raw0[:], in_=f0[c * NB : (c + 1) * NB, :].rearrange("(t p) k -> p t k", p=P)
+                    )
+                    if c == 0:
+                        prepare(raw1[:, 0:4, :], c1, s1, 0, "vs")
+                        prepare(raw1[:, 4:8, :], c1, s1, NB, "vs")
+                    prepare(raw0, c0, s0, c * NB, "vs" if cc == 0 else "ss")
+                    if g < NG - 1:
+                        row_stats(c, False)
+                col_stats(g)
+            row_stats(LC - 2, False)
+            row_stats(LC - 1, True)
+
+        NC_ = NG * ST
+        nmx = keep.tile([P, LT + ST], F32, name="nmx")
+        dd = keep.tile([P, NC_], F32, name="dd")
+        tot = keep.tile([P, LT + ST], F32, name="tot")
+        ab = keep.tile([P, LT + ST], F32, name="ab")
+        nm_c = nms[:, LT : LT + NC_].rearrange("p (g s) -> p s g", g=NG)
+        dd_c = dd[:].rearrange("p (g s) -> p s g", g=NG)
+        nc.vector.tensor_reduce(out=nmx[:, LT : LT + ST], in_=nm_c, axis=AX.X, op=ALU.min)
         nc.vector.tensor_tensor(
-            out=dd_r, in0=nmx[:, 0:32].unsqueeze(2).to_broadcast([P, LT, 2]), in1=nm_r, op=ALU.subtract
-        )
-        nc.vector.tensor_tensor(
-            out=dd_c, in0=nmx[:, 32:40].unsqueeze(2).to_broadcast([P, ST, LC]), in1=nm_c, op=ALU.subtract
+            out=dd_c, in0=nmx[:, LT : LT + ST].unsqueeze(2).to_broadcast([P, ST, NG]), in1=nm_c, op=ALU.subtract
         )
         nc.scalar.activation(out=dd[:], in_=dd[:], func=ACT.Exp)
-        nc.vector.tensor_tensor(out=dd[:], in0=dd[:], in1=sg[:], op=ALU.mult)
-        nc.vector.tensor_reduce(out=tot[:, 0:32], in_=dd_r, axis=AX.X, op=ALU.add)
-        nc.vector.tensor_reduce(out=tot[:, 32:40], in_=dd_c, axis=AX.X, op=ALU.add)
+        nc.vector.tensor_tensor(out=dd[:], in0=dd[:], in1=sums[:, LT : LT + NC_], op=ALU.mult)
+        nc.vector.tensor_reduce(out=tot[:, LT : LT + ST], in_=dd_c, axis=AX.X, op=ALU.add)
+        nc.vector.tensor_copy(out=nmx[:, 0:LT], in_=nms[:, 0:LT])
+        nc.vector.tensor_copy(out=tot[:, 0:LT], in_=sums[:, 0:LT])
         nc.scalar.activation(out=tot[:], in_=tot[:], func=ACT.Ln)
         nc.vector.tensor_tensor(out=ab[:], in0=nmx[:], in1=tot[:], op=ALU.subtract)
 
         with tc.tile_pool(name="main", bufs=1) as main:
             conf = main.tile([P, LT, S], F32, name="conf")
             best = main.tile([P, S], F32, name="best")
-            mcs = [main.tile([P, S], F32, name="mc%d" % i) for i in range(N_MC)]
-            for i in range(N_MC):
-                nc.gpsimd.memset(mcs[i][:], 0.0)
+            zero = main.tile([P, S], F32, name="zero")
+            nc.gpsimd.memset(zero[:], 0.0)
             nc.gpsimd.memset(best[:, 0:S_LO], 0.0)
             nc.gpsimd.memset(best[:, S_HI:S], 0.0)
-            nc.sync.dma_start(out=o1[0:P, :], in_=mcs[0][:])
-            nc.sync.dma_start(out=o1[L - P : L, :], in_=mcs[1][:])
+            nc.sync.dma_start(out=o1[0:P, :], in_=zero[:])
+            nc.sync.dma_start(out=o1[L - P : L, :], in_=zero[:])
+            for lo in (0, S_HI):
+                for first in (1, 16):
+                    nc.sync.dma_start(
+                        out=o1[first * P : (first + 15) * P, lo : lo + S_LO].rearrange("(j p) s -> p j s", p=P),
+                        in_=zero[:, 0 : 15 * S_LO].rearrange("p (j s) -> p j s", s=S_LO),
+                    )
             rt2 = main.tile([P, 2 * LT], F32, name="rt2")
 
-            def columns(c, w1, st):
+            def columns(c, w1, st, engine):
                 bank = psm.tile([P, NB], F32, name="bank", tag="mx")
                 mx(bank[:], c1, s1, st * P, c0, s0, c * NB)
-                nc.scalar.activation(
-                    out=w1[:, st, :],
-                    in_=bank[:],
-                    func=ACT.Identity,
-                    bias=ab[:, 32 + st : 33 + st],
-                    scale=t_two[:, 0:1],
-                )
+                if engine == "s":
+                    nc.scalar.activation(
+                        out=w1[:, st, :],
+                        in_=bank[:],
+                        func=ACT.Identity,
+                        bias=ab[:, LT + st : LT + st + 1],
+                        scale=t_two[:, 0:1],
+                    )
+                else:
+                    nc.vector.tensor_scalar(
+                        out=w1[:, st, :],
+                        in0=bank[:],
+                        scalar1=t_two[:, 0:1],
+                        scalar2=ab[:, LT + st : LT + st + 1],
+                        op0=ALU.mult,
+                        op1=ALU.add,
+                    )
 
             def rows(c, w1, j):
                 t = 4 * c + j
@@ -211,28 +268,33 @@ def tile_coarsematching_t_kernel(tc, feat_c0, feat_c1, temperature, out_0, out_1
                         op1=ALU.max,
                         accum_out=rt2[:, 2 * t + h : 2 * t + h + 1],
                     )
-                nc.scalar.activation(out=conf[:, t, :], in_=conf[:, t, :], func=ACT.Exp)
-                nc.sync.dma_start(out=o0[t * P : (t + 1) * P, :], in_=conf[:, t, :])
-                if t == 1:
-                    nc.vector.tensor_tensor(
-                        out=best[:, S_LO:S_HI], in0=conf[:, 0, S_LO:S_HI], in1=conf[:, 1, S_LO:S_HI], op=ALU.max
+                if j % 2 == 1:
+                    nc.scalar.activation(out=conf[:, t - 1 : t + 1, :], in_=conf[:, t - 1 : t + 1, :], func=ACT.Exp)
+                    nc.sync.dma_start(
+                        out=o0[(t - 1) * P : (t + 1) * P, :].rearrange("(j p) s -> p j s", p=P),
+                        in_=conf[:, t - 1 : t + 1, :],
                     )
-                elif t > 1:
-                    nc.vector.tensor_tensor(
-                        out=best[:, S_LO:S_HI], in0=best[:, S_LO:S_HI], in1=conf[:, t, S_LO:S_HI], op=ALU.max
-                    )
+                    if t == 1:
+                        nc.vector.tensor_tensor(
+                            out=best[:, S_LO:S_HI], in0=conf[:, 0, S_LO:S_HI], in1=conf[:, 1, S_LO:S_HI], op=ALU.max
+                        )
+                    else:
+                        for tt in (t - 1, t):
+                            nc.vector.tensor_tensor(
+                                out=best[:, S_LO:S_HI], in0=best[:, S_LO:S_HI], in1=conf[:, tt, S_LO:S_HI], op=ALU.max
+                            )
 
             w1_now = main.tile([P, ST, NB], F32, name="w1", tag="w1", bufs=2)
             for st in range(ST):
-                columns(0, w1_now, st)
+                columns(0, w1_now, st, "s" if st % 2 == 0 else "v")
             for c in range(LC):
                 w1_next = None
                 if c + 1 < LC:
                     w1_next = main.tile([P, ST, NB], F32, name="w1", tag="w1", bufs=2)
                 for j in range(4):
                     if c + 1 < LC:
-                        columns(c + 1, w1_next, 2 * j)
-                        columns(c + 1, w1_next, 2 * j + 1)
+                        columns(c + 1, w1_next, 2 * j, "s")
+                        columns(c + 1, w1_next, 2 * j + 1, "s")
                     rows(c, w1_now, j)
                 w1_now = w1_next
 
@@ -261,9 +323,9 @@ def tile_coarsematching_t_kernel(tc, feat_c0, feat_c1, temperature, out_0, out_1
                     nc.tensor.transpose(cb[:, q * P : (q + 1) * P], spread[:, 4 * h + q, :], ident[:])
                 cbs.append(cb)
 
-            half = (S_HI - S_LO) // 2
+            half = S_IN // 2
             for t in range(1, LT - 1):
-                mask = main.tile([P, S_HI - S_LO], BF16, name="mask", tag="mask", bufs=3)
+                mask = main.tile([P, S_IN], BF16, name="mask", tag="mask", bufs=3)
                 nc.vector.scalar_tensor_tensor(
                     out=mask[:, 0:half],
                     in0=cbs[0][:, S_LO:NB],
@@ -273,13 +335,13 @@ def tile_coarsematching_t_kernel(tc, feat_c0, feat_c1, temperature, out_0, out_1
                     op1=ALU.is_equal,
                 )
                 nc.vector.scalar_tensor_tensor(
-                    out=mask[:, half : 2 * half],
+                    out=mask[:, half:S_IN],
                     in0=cbs[1][:, 0 : S_HI - NB],
                     scalar=rgate[:, t : t + 1],
                     in1=conf[:, t, NB:S_HI],
                     op0=ALU.max,
                     op1=ALU.is_equal,
                 )
-                mc = mcs[t % N_MC]
-                nc.scalar.activation(out=mc[:, S_LO:S_HI], in_=mask[:], func=ACT.Copy, scale=rmax[:, t : t + 1])
-                nc.sync.dma_start(out=o1[t * P : (t + 1) * P, :], in_=mc[:])
+                mc = main.tile([P, S_IN], F32, name="mc", tag="mc", bufs=N_MC)
+                nc.scalar.activation(out=mc[:], in_=mask[:], func=ACT.Copy, scale=rmax[:, t : t + 1])
+                nc.sync.dma_start(out=o1[t * P : (t + 1) * P, S_LO:S_HI], in_=mc[:])

@@ -36,18 +36,130 @@ def tile_coarsematching_t_kernel(tc, feat_c0, feat_c1, temperature, out_0, out_1
     o0 = out_0.flatten_outer_dims()
     o1 = out_1.flatten_outer_dims()
 
-    with tc.tile_pool(name="keep", bufs=1) as keep, tc.psum_pool(name="psm", bufs=5) as psm, tc.psum_pool(
-        name="pst", bufs=3
-    ) as pst:
+    with tc.tile_pool(name="keep", bufs=1) as keep, tc.tile_pool(name="junk", bufs=3) as junk, tc.psum_pool(
+        name="psm", bufs=5
+    ) as psm, tc.psum_pool(name="pst", bufs=3) as pst:
         ident = keep.tile([P, P], F32, name="ident")
         make_identity(nc, ident[:])
 
         t_bf = keep.tile([P, 1], BF16, name="t_bf")
         nc.sync.dma_start(out=t_bf[:], in_=temperature.partition_broadcast(P))
+        t_pos = keep.tile([P, 1], F32, name="t_pos")
         t_neg = keep.tile([P, 1], F32, name="t_neg")
         t_two = keep.tile([P, 1], F32, name="t_two")
+        nc.vector.tensor_copy(out=t_pos[:], in_=t_bf[:])
         nc.vector.tensor_scalar(out=t_neg[:], in0=t_bf[:], scalar1=-1.0, scalar2=None, op0=ALU.mult)
         nc.vector.tensor_scalar(out=t_two[:], in0=t_bf[:], scalar1=2.0, scalar2=None, op0=ALU.mult)
+
+        c0 = keep.tile([P, L], U32, name="c0", align_bytes=64)
+        s0 = keep.tile([P, L], U8, name="s0", align_bytes=64)
+        c1 = keep.tile([P, S], U32, name="c1", align_bytes=64)
+        s1 = keep.tile([P, S], U8, name="s1", align_bytes=64)
+
+        nm_c = keep.tile([P, ST * LC], F32, name="nm_c")
+        sg_c = keep.tile([P, ST * LC], F32, name="sg_c")
+        nm_b = keep.tile([P, 2 * LT], F32, name="nm_b")
+        nm_r = keep.tile([P, LT], F32, name="nm_r")
+        sg_b = keep.tile([P, 2 * LT], F32, name="sg_b")
+        r_inv = keep.tile([P, LT], F32, name="r_inv")
+        rmax = keep.tile([P, LT], F32, name="rmax")
+
+        def mx(bank, codes_a, scales_a, a_lo, codes_b, scales_b, b_lo):
+            nc.tensor.matmul_mx(
+                out=bank,
+                lhsT=codes_a[:, a_lo : a_lo + P].bitcast(FP8X4),
+                lhsT_scale=scales_a[:, a_lo : a_lo + P],
+                rhs=codes_b[:, b_lo : b_lo + NB].bitcast(FP8X4),
+                rhs_scale=scales_b[:, b_lo : b_lo + NB],
+                start=True,
+                stop=True,
+            )
+
+        def neg_max(bank, nm_col):
+            jv = junk.tile([P, NB], BF16, name="jv", tag="jv")
+            nc.vector.tensor_scalar(
+                out=jv[:], in0=bank, scalar1=t_neg[:, 0:1], scalar2=None, op0=ALU.mult, op1=ALU.min, accum_out=nm_col
+            )
+
+        def exp_sum(bank, nm_col, sg_col):
+            js = junk.tile([P, NB], BF16, name="js", tag="js")
+            nc.scalar.activation(
+                out=js[:], in_=bank, func=ACT.Exp, bias=nm_col, scale=t_pos[:, 0:1], accum_out=sg_col
+            )
+
+        def col_unit(st, c):
+            col = LC * st + c
+            bank = psm.tile([P, NB], F32, name="bank", tag="mx")
+            mx(bank[:], c1, s1, st * P, c0, s0, c * NB)
+            neg_max(bank[:], nm_c[:, col : col + 1])
+            exp_sum(bank[:], nm_c[:, col : col + 1], sg_c[:, col : col + 1])
+
+        def row_unit(t):
+            banks = []
+            for h in range(2):
+                bank = psm.tile([P, NB], F32, name="bank", tag="mx")
+                mx(bank[:], c0, s0, t * P, c1, s1, h * NB)
+                neg_max(bank[:], nm_b[:, 2 * t + h : 2 * t + h + 1])
+                banks.append(bank)
+            nc.vector.tensor_tensor(
+                out=nm_r[:, t : t + 1], in0=nm_b[:, 2 * t : 2 * t + 1], in1=nm_b[:, 2 * t + 1 : 2 * t + 2], op=ALU.min
+            )
+            for h in range(2):
+                exp_sum(banks[h][:], nm_r[:, t : t + 1], sg_b[:, 2 * t + h : 2 * t + h + 1])
+
+        def row_norm(t_lo, n):
+            nc.vector.tensor_reduce(
+                out=r_inv[:, t_lo : t_lo + n],
+                in_=sg_b[:, 2 * t_lo : 2 * (t_lo + n)].rearrange("p (t h) -> p t h", h=2),
+                axis=AX.X,
+                op=ALU.add,
+            )
+            nc.vector.reciprocal(out=r_inv[:, t_lo : t_lo + n], in_=r_inv[:, t_lo : t_lo + n])
+
+        with tc.tile_pool(name="head", bufs=3) as head:
+
+            def prepare(raw, codes, scales, lo):
+                grouped = head.tile([P, NB, 4], BF16, name="grouped", tag="grouped", align_bytes=64)
+                for half in range(2):
+                    bank = pst.tile([P, 2, 256], F32, name="tbank", tag="tr")
+                    for i in range(2):
+                        words = raw[:, 2 * half + i, :].bitcast(F32)
+                        for u in range(2):
+                            nc.tensor.transpose(
+                                bank[:, u, P * i : P * (i + 1)], words[:, P * u : P * (u + 1)], ident[:]
+                            )
+                    src = bank[:].bitcast(BF16).rearrange("p u (l e) -> p l u e", e=2)
+                    dst = grouped[:, 256 * half : 256 * (half + 1), :].rearrange("p l (u e) -> p l u e", e=2)
+                    if half == 0:
+                        nc.vector.tensor_scalar(out=dst, in0=src, scalar1=INV_SQRT_C, scalar2=None, op0=ALU.mult)
+                    else:
+                        nc.scalar.activation(out=dst, in_=src, func=ACT.Copy, scale=INV_SQRT_C)
+                nc.vector.quantize_mx(
+                    out=codes[:, lo : lo + NB].bitcast(FP8X4),
+                    scales=scales[:, lo : lo + NB],
+                    in_=grouped[:].rearrange("p l j -> p (l j)"),
+                )
+
+            def load(src_rows):
+                raw = head.tile([P, 4, C], BF16, name="raw", tag="raw", bufs=4)
+                nc.sync.dma_start(out=raw[:], in_=src_rows.rearrange("(t p) k -> p t k", p=P))
+                return raw
+
+            raw_1a = load(f1[0:NB, :])
+            raw_0 = load(f0[0:NB, :])
+            raw_1b = load(f1[NB:S, :])
+            prepare(raw_1a, c1, s1, 0)
+            prepare(raw_0, c0, s0, 0)
+            for st in range(4):
+                col_unit(st, 0)
+            prepare(raw_1b, c1, s1, NB)
+            for st in range(4, ST):
+                col_unit(st, 0)
+            for c in range(1, LC):
+                raw_0 = load(f0[c * NB : (c + 1) * NB, :])
+                prepare(raw_0, c0, s0, c * NB)
+                for st in range(ST):
+                    col_unit(st, c)
 
         edge = keep.tile([P, 4], F32, name="edge")
         id64 = ident[:].rearrange("p (a b) -> p a b", b=64)
@@ -63,155 +175,25 @@ def tile_coarsematching_t_kernel(tc, feat_c0, feat_c1, temperature, out_0, out_1
         nc.vector.tensor_scalar(out=row_edge[:], in0=row_edge[:], scalar1=NEVER, scalar2=None, op0=ALU.mult)
         nc.vector.tensor_scalar(out=col_edge[:], in0=col_edge[:], scalar1=NEVER, scalar2=None, op0=ALU.mult)
 
-        c0 = keep.tile([P, L], U32, name="c0", align_bytes=64)
-        s0 = keep.tile([P, L], U8, name="s0", align_bytes=64)
-        c1 = keep.tile([P, S], U32, name="c1", align_bytes=64)
-        s1 = keep.tile([P, S], U8, name="s1", align_bytes=64)
-
-        NG = LC // 2
-        nm_bank_r = keep.tile([P, 2 * LT], F32, name="nm_bank_r")
-        nm_bank_c = keep.tile([P, NG, ST, 2], F32, name="nm_bank_c")
-        nms = keep.tile([P, LT + NG * ST], F32, name="nms")
-        sums = keep.tile([P, LT + NG * ST], F32, name="sums")
-
-        def mx(bank, codes_a, scales_a, a_lo, codes_b, scales_b, b_lo):
-            nc.tensor.matmul_mx(
-                out=bank,
-                lhsT=codes_a[:, a_lo : a_lo + P].bitcast(FP8X4),
-                lhsT_scale=scales_a[:, a_lo : a_lo + P],
-                rhs=codes_b[:, b_lo : b_lo + NB].bitcast(FP8X4),
-                rhs_scale=scales_b[:, b_lo : b_lo + NB],
-                start=True,
-                stop=True,
-            )
-
-        def negated(dst, nm_col, codes_a, scales_a, a_lo, codes_b, scales_b, b_lo):
-            bank = psm.tile([P, NB], F32, name="bank", tag="mx")
-            mx(bank[:], codes_a, scales_a, a_lo, codes_b, scales_b, b_lo)
-            nc.vector.tensor_scalar(
-                out=dst,
-                in0=bank[:],
-                scalar1=t_neg[:, 0:1],
-                scalar2=None,
-                op0=ALU.mult,
-                op1=ALU.min,
-                accum_out=nm_col,
-            )
-
-        with tc.tile_pool(name="head", bufs=3) as head, tc.tile_pool(name="stage", bufs=2) as stage:
-
-            def exp_sum(src, col):
-                js = stage.tile([P, 2 * NB], BF16, name="js", tag="js")
-                nc.scalar.activation(
-                    out=js[:],
-                    in_=src,
-                    func=ACT.Exp,
-                    bias=nms[:, col : col + 1],
-                    scale=-1.0,
-                    accum_out=sums[:, col : col + 1],
-                )
-
-            def prepare(raw, codes, scales, lo, engines):
-                grouped = head.tile([P, NB, 4], BF16, name="grouped", tag="grouped", align_bytes=64)
-                for half in range(2):
-                    bank = pst.tile([P, 2, 256], F32, name="tbank", tag="tr")
-                    for i in range(2):
-                        words = raw[:, 2 * half + i, :].bitcast(F32)
-                        for u in range(2):
-                            nc.tensor.transpose(
-                                bank[:, u, P * i : P * (i + 1)], words[:, P * u : P * (u + 1)], ident[:]
-                            )
-                    src = bank[:].bitcast(BF16).rearrange("p u (l e) -> p l u e", e=2)
-                    dst = grouped[:, 256 * half : 256 * (half + 1), :].rearrange("p l (u e) -> p l u e", e=2)
-                    if engines[half] == "v":
-                        nc.vector.tensor_scalar(out=dst, in0=src, scalar1=INV_SQRT_C, scalar2=None, op0=ALU.mult)
-                    else:
-                        nc.scalar.activation(out=dst, in_=src, func=ACT.Copy, scale=INV_SQRT_C)
-                nc.vector.quantize_mx(
-                    out=codes[:, lo : lo + NB].bitcast(FP8X4),
-                    scales=scales[:, lo : lo + NB],
-                    in_=grouped[:].rearrange("p l j -> p (l j)"),
-                )
-
-            def row_stats(c, per_tile):
-                nxr = stage.tile([P, 4, S], F32, name="nxr", tag="nxr")
-                for j in range(4):
-                    t = 4 * c + j
-                    for h in range(2):
-                        negated(
-                            nxr[:, j, h * NB : (h + 1) * NB],
-                            nm_bank_r[:, 2 * t + h : 2 * t + h + 1],
-                            c0, s0, t * P, c1, s1, h * NB,
-                        )
-                    if per_tile:
-                        nc.vector.tensor_tensor(
-                            out=nms[:, t : t + 1],
-                            in0=nm_bank_r[:, 2 * t : 2 * t + 1],
-                            in1=nm_bank_r[:, 2 * t + 1 : 2 * t + 2],
-                            op=ALU.min,
-                        )
-                        exp_sum(nxr[:, j, :], t)
-                if not per_tile:
-                    nc.vector.tensor_reduce(
-                        out=nms[:, 4 * c : 4 * c + 4],
-                        in_=nm_bank_r[:, 8 * c : 8 * c + 8].rearrange("p (t h) -> p t h", h=2),
-                        axis=AX.X,
-                        op=ALU.min,
-                    )
-                    for j in range(4):
-                        exp_sum(nxr[:, j, :], 4 * c + j)
-
-            def col_stats(g):
-                nxc = stage.tile([P, ST, 2 * NB], F32, name="nxc", tag="nxc")
-                for st in range(ST):
-                    for cc in range(2):
-                        negated(
-                            nxc[:, st, cc * NB : (cc + 1) * NB],
-                            nm_bank_c[:, g, st, cc : cc + 1],
-                            c1, s1, st * P, c0, s0, (2 * g + cc) * NB,
-                        )
-                lo = LT + g * ST
-                nc.vector.tensor_reduce(out=nms[:, lo : lo + ST], in_=nm_bank_c[:, g, :, :], axis=AX.X, op=ALU.min)
-                for st in range(ST):
-                    exp_sum(nxc[:, st, :], lo + st)
-
-            raw1 = head.tile([P, ST, C], BF16, name="raw1", tag="raw1", bufs=1)
-            nc.sync.dma_start(out=raw1[:], in_=f1.rearrange("(t p) k -> p t k", p=P))
-            for g in range(NG):
-                for cc in range(2):
-                    c = 2 * g + cc
-                    raw0 = head.tile([P, 4, C], BF16, name="raw0", tag="raw0")
-                    nc.sync.dma_start(
-                        out=raw0[:], in_=f0[c * NB : (c + 1) * NB, :].rearrange("(t p) k -> p t k", p=P)
-                    )
-                    if c == 0:
-                        prepare(raw1[:, 0:4, :], c1, s1, 0, "vs")
-                        prepare(raw1[:, 4:8, :], c1, s1, NB, "vs")
-                    prepare(raw0, c0, s0, c * NB, "vs" if cc == 0 else "ss")
-                    if g < NG - 1:
-                        row_stats(c, False)
-                col_stats(g)
-            row_stats(LC - 2, False)
-            row_stats(LC - 1, True)
-
-        NC_ = NG * ST
-        nmx = keep.tile([P, LT + ST], F32, name="nmx")
-        dd = keep.tile([P, NC_], F32, name="dd")
-        tot = keep.tile([P, LT + ST], F32, name="tot")
-        ab = keep.tile([P, LT + ST], F32, name="ab")
-        nm_c = nms[:, LT : LT + NC_].rearrange("p (g s) -> p s g", g=NG)
-        dd_c = dd[:].rearrange("p (g s) -> p s g", g=NG)
-        nc.vector.tensor_reduce(out=nmx[:, LT : LT + ST], in_=nm_c, axis=AX.X, op=ALU.min)
+        nmx = keep.tile([P, ST], F32, name="nmx")
+        dd = keep.tile([P, ST * LC], F32, name="dd")
+        tot = keep.tile([P, ST], F32, name="tot")
+        b_col = keep.tile([P, ST], F32, name="b_col")
+        nm_c3 = nm_c[:].rearrange("p (s c) -> p s c", c=LC)
+        dd3 = dd[:].rearrange("p (s c) -> p s c", c=LC)
+        nc.vector.tensor_reduce(out=nmx[:], in_=nm_c3, axis=AX.X, op=ALU.min)
         nc.vector.tensor_tensor(
-            out=dd_c, in0=nmx[:, LT : LT + ST].unsqueeze(2).to_broadcast([P, ST, NG]), in1=nm_c, op=ALU.subtract
+            out=dd3, in0=nmx[:].unsqueeze(2).to_broadcast([P, ST, LC]), in1=nm_c3, op=ALU.subtract
         )
         nc.scalar.activation(out=dd[:], in_=dd[:], func=ACT.Exp)
-        nc.vector.tensor_tensor(out=dd[:], in0=dd[:], in1=sums[:, LT : LT + NC_], op=ALU.mult)
-        nc.vector.tensor_reduce(out=tot[:, LT : LT + ST], in_=dd_c, axis=AX.X, op=ALU.add)
-        nc.vector.tensor_copy(out=nmx[:, 0:LT], in_=nms[:, 0:LT])
-        nc.vector.tensor_copy(out=tot[:, 0:LT], in_=sums[:, 0:LT])
+        nc.vector.tensor_tensor(out=dd[:], in0=dd[:], in1=sg_c[:], op=ALU.mult)
+        nc.vector.tensor_reduce(out=tot[:], in_=dd3, axis=AX.X, op=ALU.add)
         nc.scalar.activation(out=tot[:], in_=tot[:], func=ACT.Ln)
-        nc.vector.tensor_tensor(out=ab[:], in0=nmx[:], in1=tot[:], op=ALU.subtract)
+        nc.vector.tensor_tensor(out=b_col[:], in0=nmx[:], in1=tot[:], op=ALU.subtract)
+
+        for t in range(4):
+            row_unit(t)
+        row_norm(0, 4)
 
         with tc.tile_pool(name="main", bufs=1) as main:
             conf = main.tile([P, LT, S], F32, name="conf")
@@ -228,28 +210,13 @@ def tile_coarsematching_t_kernel(tc, feat_c0, feat_c1, temperature, out_0, out_1
                         out=o1[first * P : (first + 15) * P, lo : lo + S_LO].rearrange("(j p) s -> p j s", p=P),
                         in_=zero[:, 0 : 15 * S_LO].rearrange("p (j s) -> p j s", s=S_LO),
                     )
-            rt2 = main.tile([P, 2 * LT], F32, name="rt2")
 
-            def columns(c, w1, st, engine):
+            def columns(c, w1, st):
                 bank = psm.tile([P, NB], F32, name="bank", tag="mx")
                 mx(bank[:], c1, s1, st * P, c0, s0, c * NB)
-                if engine == "s":
-                    nc.scalar.activation(
-                        out=w1[:, st, :],
-                        in_=bank[:],
-                        func=ACT.Identity,
-                        bias=ab[:, LT + st : LT + st + 1],
-                        scale=t_two[:, 0:1],
-                    )
-                else:
-                    nc.vector.tensor_scalar(
-                        out=w1[:, st, :],
-                        in0=bank[:],
-                        scalar1=t_two[:, 0:1],
-                        scalar2=ab[:, LT + st : LT + st + 1],
-                        op0=ALU.mult,
-                        op1=ALU.add,
-                    )
+                nc.scalar.activation(
+                    out=w1[:, st, :], in_=bank[:], func=ACT.Identity, bias=b_col[:, st : st + 1], scale=t_two[:, 0:1]
+                )
 
             def rows(c, w1, j):
                 t = 4 * c + j
@@ -259,49 +226,46 @@ def tile_coarsematching_t_kernel(tc, feat_c0, feat_c1, temperature, out_0, out_1
                         nc.tensor.transpose(
                             tb[:, q * P : (q + 1) * P], w1[:, 4 * h + q, j * P : (j + 1) * P], ident[:]
                         )
-                    nc.vector.tensor_scalar(
-                        out=conf[:, t, h * NB : (h + 1) * NB],
-                        in0=tb[:],
-                        scalar1=ab[:, t : t + 1],
-                        scalar2=None,
-                        op0=ALU.add,
-                        op1=ALU.max,
-                        accum_out=rt2[:, 2 * t + h : 2 * t + h + 1],
+                    nc.scalar.activation(
+                        out=conf[:, t, h * NB : (h + 1) * NB], in_=tb[:], func=ACT.Exp, bias=nm_r[:, t : t + 1]
                     )
-                if j % 2 == 1:
-                    nc.scalar.activation(out=conf[:, t - 1 : t + 1, :], in_=conf[:, t - 1 : t + 1, :], func=ACT.Exp)
-                    nc.sync.dma_start(
-                        out=o0[(t - 1) * P : (t + 1) * P, :].rearrange("(j p) s -> p j s", p=P),
-                        in_=conf[:, t - 1 : t + 1, :],
+                nc.vector.tensor_scalar(
+                    out=conf[:, t, :],
+                    in0=conf[:, t, :],
+                    scalar1=r_inv[:, t : t + 1],
+                    scalar2=None,
+                    op0=ALU.mult,
+                    op1=ALU.max,
+                    accum_out=rmax[:, t : t + 1],
+                )
+                nc.sync.dma_start(out=o0[t * P : (t + 1) * P, :], in_=conf[:, t, :])
+                if t == 1:
+                    nc.vector.tensor_tensor(
+                        out=best[:, S_LO:S_HI], in0=conf[:, 0, S_LO:S_HI], in1=conf[:, 1, S_LO:S_HI], op=ALU.max
                     )
-                    if t == 1:
-                        nc.vector.tensor_tensor(
-                            out=best[:, S_LO:S_HI], in0=conf[:, 0, S_LO:S_HI], in1=conf[:, 1, S_LO:S_HI], op=ALU.max
-                        )
-                    else:
-                        for tt in (t - 1, t):
-                            nc.vector.tensor_tensor(
-                                out=best[:, S_LO:S_HI], in0=best[:, S_LO:S_HI], in1=conf[:, tt, S_LO:S_HI], op=ALU.max
-                            )
+                elif t > 1:
+                    nc.vector.tensor_tensor(
+                        out=best[:, S_LO:S_HI], in0=best[:, S_LO:S_HI], in1=conf[:, t, S_LO:S_HI], op=ALU.max
+                    )
 
             w1_now = main.tile([P, ST, NB], F32, name="w1", tag="w1", bufs=2)
             for st in range(ST):
-                columns(0, w1_now, st, "s" if st % 2 == 0 else "v")
+                columns(0, w1_now, st)
             for c in range(LC):
                 w1_next = None
                 if c + 1 < LC:
                     w1_next = main.tile([P, ST, NB], F32, name="w1", tag="w1", bufs=2)
                 for j in range(4):
                     if c + 1 < LC:
-                        columns(c + 1, w1_next, 2 * j, "s")
-                        columns(c + 1, w1_next, 2 * j + 1, "s")
+                        row_unit(4 * (c + 1) + j)
+                        columns(c + 1, w1_next, 2 * j)
+                        columns(c + 1, w1_next, 2 * j + 1)
                     rows(c, w1_now, j)
+                if c + 1 < LC:
+                    row_norm(4 * (c + 1), 4)
                 w1_now = w1_next
 
-            rmax = main.tile([P, LT], F32, name="rmax")
             rgate = main.tile([P, LT], F32, name="rgate")
-            nc.vector.tensor_reduce(out=rmax[:], in_=rt2[:].rearrange("p (t h) -> p t h", h=2), axis=AX.X, op=ALU.max)
-            nc.scalar.activation(out=rmax[:], in_=rmax[:], func=ACT.Exp)
             nc.vector.tensor_scalar(out=rgate[:], in0=rmax[:], scalar1=THR, scalar2=NEVER, op0=ALU.is_le, op1=ALU.mult)
             nc.vector.tensor_tensor(out=rgate[:], in0=rgate[:], in1=rmax[:], op=ALU.max)
             nc.vector.tensor_scalar(out=rgate[:], in0=rgate[:], scalar1=row_edge[:, 0:1], scalar2=None, op0=ALU.max)

@@ -24,7 +24,6 @@ NEVER = 2.0
 S_LO = 64
 S_HI = 960
 S_IN = S_HI - S_LO
-N_MC = 4
 
 FLOPS = 2 * L * S * C
 
@@ -36,20 +35,14 @@ def tile_coarsematching_t_kernel(tc, feat_c0, feat_c1, temperature, out_0, out_1
     o0 = out_0.flatten_outer_dims()
     o1 = out_1.flatten_outer_dims()
 
-    with tc.tile_pool(name="keep", bufs=1) as keep, tc.tile_pool(name="junk", bufs=3) as junk, tc.psum_pool(
-        name="psm", bufs=5
-    ) as psm, tc.psum_pool(name="pst", bufs=3) as pst:
+    with tc.manual_schedule(), tc.tile_pool(name="keep", bufs=1) as keep, tc.tile_pool(
+        name="junk", bufs=2
+    ) as junk, tc.psum_pool(name="psm", bufs=4) as psm, tc.psum_pool(name="pst", bufs=4) as pst:
         ident = keep.tile([P, P], F32, name="ident")
         make_identity(nc, ident[:])
 
         t_bf = keep.tile([P, 1], BF16, name="t_bf")
         nc.sync.dma_start(out=t_bf[:], in_=temperature.partition_broadcast(P))
-        t_pos = keep.tile([P, 1], F32, name="t_pos")
-        t_neg = keep.tile([P, 1], F32, name="t_neg")
-        t_two = keep.tile([P, 1], F32, name="t_two")
-        nc.vector.tensor_copy(out=t_pos[:], in_=t_bf[:])
-        nc.vector.tensor_scalar(out=t_neg[:], in0=t_bf[:], scalar1=-1.0, scalar2=None, op0=ALU.mult)
-        nc.vector.tensor_scalar(out=t_two[:], in0=t_bf[:], scalar1=2.0, scalar2=None, op0=ALU.mult)
 
         c0 = keep.tile([P, L], U32, name="c0", align_bytes=64)
         s0 = keep.tile([P, L], U8, name="s0", align_bytes=64)
@@ -60,9 +53,15 @@ def tile_coarsematching_t_kernel(tc, feat_c0, feat_c1, temperature, out_0, out_1
         sg_c = keep.tile([P, ST * LC], F32, name="sg_c")
         nm_b = keep.tile([P, 2 * LT], F32, name="nm_b")
         nm_r = keep.tile([P, LT], F32, name="nm_r")
-        sg_b = keep.tile([P, 2 * LT], F32, name="sg_b")
+        rsum = keep.tile([P, LT], F32, name="rsum")
         r_inv = keep.tile([P, LT], F32, name="r_inv")
         rmax = keep.tile([P, LT], F32, name="rmax")
+        t_pos = keep.tile([P, 1], F32, name="t_pos")
+        t_neg = keep.tile([P, 1], F32, name="t_neg")
+        t_two = keep.tile([P, 1], F32, name="t_two")
+        edge = keep.tile([P, 4], F32, name="edge")
+        row_edge = keep.tile([P, 1], F32, name="row_edge")
+        col_edge = keep.tile([P, 1], F32, name="col_edge")
 
         def mx(bank, codes_a, scales_a, a_lo, codes_b, scales_b, b_lo):
             nc.tensor.matmul_mx(
@@ -75,50 +74,87 @@ def tile_coarsematching_t_kernel(tc, feat_c0, feat_c1, temperature, out_0, out_1
                 stop=True,
             )
 
-        def neg_max(bank, nm_col):
-            jv = junk.tile([P, NB], BF16, name="jv", tag="jv")
+        def neg_max(dst, bank, nm_col):
             nc.vector.tensor_scalar(
-                out=jv[:], in0=bank, scalar1=t_neg[:, 0:1], scalar2=None, op0=ALU.mult, op1=ALU.min, accum_out=nm_col
-            )
-
-        def exp_sum(bank, nm_col, sg_col):
-            js = junk.tile([P, NB], BF16, name="js", tag="js")
-            nc.scalar.activation(
-                out=js[:], in_=bank, func=ACT.Exp, bias=nm_col, scale=t_pos[:, 0:1], accum_out=sg_col
+                out=dst, in0=bank, scalar1=t_neg[:, 0:1], scalar2=None, op0=ALU.mult, op1=ALU.min, accum_out=nm_col
             )
 
         def col_unit(st, c):
             col = LC * st + c
             bank = psm.tile([P, NB], F32, name="bank", tag="mx")
             mx(bank[:], c1, s1, st * P, c0, s0, c * NB)
-            neg_max(bank[:], nm_c[:, col : col + 1])
-            exp_sum(bank[:], nm_c[:, col : col + 1], sg_c[:, col : col + 1])
+            jv = junk.tile([P, NB], BF16, name="jv", tag="jv")
+            neg_max(jv[:], bank[:], nm_c[:, col : col + 1])
+            js = junk.tile([P, NB], BF16, name="js", tag="js")
+            nc.scalar.activation(
+                out=js[:],
+                in_=bank[:],
+                func=ACT.Exp,
+                bias=nm_c[:, col : col + 1],
+                scale=t_pos[:, 0:1],
+                accum_out=sg_c[:, col : col + 1],
+            )
 
-        def row_unit(t):
-            banks = []
+        nxs = {}
+
+        def row_front(t):
+            nx = junk.tile([P, S], F32, name="nx", tag="nx", bufs=3)
             for h in range(2):
                 bank = psm.tile([P, NB], F32, name="bank", tag="mx")
                 mx(bank[:], c0, s0, t * P, c1, s1, h * NB)
-                neg_max(bank[:], nm_b[:, 2 * t + h : 2 * t + h + 1])
-                banks.append(bank)
+                neg_max(nx[:, h * NB : (h + 1) * NB], bank[:], nm_b[:, 2 * t + h : 2 * t + h + 1])
             nc.vector.tensor_tensor(
                 out=nm_r[:, t : t + 1], in0=nm_b[:, 2 * t : 2 * t + 1], in1=nm_b[:, 2 * t + 1 : 2 * t + 2], op=ALU.min
             )
-            for h in range(2):
-                exp_sum(banks[h][:], nm_r[:, t : t + 1], sg_b[:, 2 * t + h : 2 * t + h + 1])
+            nxs[t] = nx
 
-        def row_norm(t_lo, n):
-            nc.vector.tensor_reduce(
-                out=r_inv[:, t_lo : t_lo + n],
-                in_=sg_b[:, 2 * t_lo : 2 * (t_lo + n)].rearrange("p (t h) -> p t h", h=2),
-                axis=AX.X,
-                op=ALU.add,
+        def row_exp(t):
+            nx = nxs[t]
+            nc.scalar.activation(
+                out=nx[:], in_=nx[:], func=ACT.Exp, bias=nm_r[:, t : t + 1], scale=-1.0, accum_out=rsum[:, t : t + 1]
             )
-            nc.vector.reciprocal(out=r_inv[:, t_lo : t_lo + n], in_=r_inv[:, t_lo : t_lo + n])
+
+        def row_recip(t):
+            nc.vector.reciprocal(out=r_inv[:, t : t + 1], in_=rsum[:, t : t + 1])
 
         with tc.tile_pool(name="head", bufs=3) as head:
+            zero = head.tile([P, S], F32, name="zero", bufs=1)
+            nc.gpsimd.memset(zero[:], 0.0)
 
-            def prepare(raw, codes, scales, lo):
+            def load(src_rows, name):
+                raw = head.tile([P, 4, C], BF16, name=name, bufs=1)
+                nc.sync.dma_start(out=raw[:], in_=src_rows.rearrange("(t p) k -> p t k", p=P))
+                return raw
+
+            raw_1a = load(f1[0:NB, :], "raw_1a")
+            raw_0 = [load(f0[0:NB, :], "raw_00")]
+            raw_1b = load(f1[NB:S, :], "raw_1b")
+            for c in range(1, LC):
+                raw_0.append(load(f0[c * NB : (c + 1) * NB, :], "raw_0%d" % c))
+            nc.sync.dma_start(out=o1[0:P, :], in_=zero[:])
+            nc.sync.dma_start(out=o1[L - P : L, :], in_=zero[:])
+            for lo in (0, S_HI):
+                for first in (1, 16):
+                    nc.sync.dma_start(
+                        out=o1[first * P : (first + 15) * P, lo : lo + S_LO].rearrange("(j p) s -> p j s", p=P),
+                        in_=zero[:, 0 : 15 * S_LO].rearrange("p (j s) -> p j s", s=S_LO),
+                    )
+
+            nc.vector.tensor_copy(out=t_pos[:], in_=t_bf[:])
+            nc.vector.tensor_scalar(out=t_neg[:], in0=t_bf[:], scalar1=-1.0, scalar2=None, op0=ALU.mult)
+            nc.vector.tensor_scalar(out=t_two[:], in0=t_bf[:], scalar1=2.0, scalar2=None, op0=ALU.mult)
+            id64 = ident[:].rearrange("p (a b) -> p a b", b=64)
+            id32 = ident[:].rearrange("p (a b) -> p a b", b=32)
+            nc.vector.tensor_reduce(out=edge[:, 0:1], in_=id64[:, :, 0:2], axis=AX.XY, op=ALU.add)
+            nc.vector.tensor_reduce(out=edge[:, 1:2], in_=id64[:, :, 62:64], axis=AX.XY, op=ALU.add)
+            nc.vector.tensor_reduce(out=edge[:, 2:3], in_=id32[:, :, 0:2], axis=AX.XY, op=ALU.add)
+            nc.vector.tensor_reduce(out=edge[:, 3:4], in_=id32[:, :, 30:32], axis=AX.XY, op=ALU.add)
+            nc.vector.tensor_tensor(out=row_edge[:], in0=edge[:, 0:1], in1=edge[:, 1:2], op=ALU.add)
+            nc.vector.tensor_tensor(out=col_edge[:], in0=edge[:, 2:3], in1=edge[:, 3:4], op=ALU.add)
+            nc.vector.tensor_scalar(out=row_edge[:], in0=row_edge[:], scalar1=NEVER, scalar2=None, op0=ALU.mult)
+            nc.vector.tensor_scalar(out=col_edge[:], in0=col_edge[:], scalar1=NEVER, scalar2=None, op0=ALU.mult)
+
+            def turn(raw, engines):
                 grouped = head.tile([P, NB, 4], BF16, name="grouped", tag="grouped", align_bytes=64)
                 for half in range(2):
                     bank = pst.tile([P, 2, 256], F32, name="tbank", tag="tr")
@@ -130,50 +166,36 @@ def tile_coarsematching_t_kernel(tc, feat_c0, feat_c1, temperature, out_0, out_1
                             )
                     src = bank[:].bitcast(BF16).rearrange("p u (l e) -> p l u e", e=2)
                     dst = grouped[:, 256 * half : 256 * (half + 1), :].rearrange("p l (u e) -> p l u e", e=2)
-                    if half == 0:
+                    if engines[half] == "v":
                         nc.vector.tensor_scalar(out=dst, in0=src, scalar1=INV_SQRT_C, scalar2=None, op0=ALU.mult)
                     else:
                         nc.scalar.activation(out=dst, in_=src, func=ACT.Copy, scale=INV_SQRT_C)
+                return grouped
+
+            def quantise(grouped, codes, scales, lo):
                 nc.vector.quantize_mx(
                     out=codes[:, lo : lo + NB].bitcast(FP8X4),
                     scales=scales[:, lo : lo + NB],
                     in_=grouped[:].rearrange("p l j -> p (l j)"),
                 )
 
-            def load(src_rows):
-                raw = head.tile([P, 4, C], BF16, name="raw", tag="raw", bufs=4)
-                nc.sync.dma_start(out=raw[:], in_=src_rows.rearrange("(t p) k -> p t k", p=P))
-                return raw
-
-            raw_1a = load(f1[0:NB, :])
-            raw_0 = load(f0[0:NB, :])
-            raw_1b = load(f1[NB:S, :])
-            prepare(raw_1a, c1, s1, 0)
-            prepare(raw_0, c0, s0, 0)
-            for st in range(4):
-                col_unit(st, 0)
-            prepare(raw_1b, c1, s1, NB)
-            for st in range(4, ST):
-                col_unit(st, 0)
-            for c in range(1, LC):
-                raw_0 = load(f0[c * NB : (c + 1) * NB, :])
-                prepare(raw_0, c0, s0, c * NB)
-                for st in range(ST):
+            g_1a = turn(raw_1a, "vs")
+            g_0 = turn(raw_0[0], "vs")
+            quantise(g_1a, c1, s1, 0)
+            g_1b = turn(raw_1b, "vs")
+            quantise(g_0, c0, s0, 0)
+            for c in range(LC):
+                for st in range(4):
                     col_unit(st, c)
-
-        edge = keep.tile([P, 4], F32, name="edge")
-        id64 = ident[:].rearrange("p (a b) -> p a b", b=64)
-        id32 = ident[:].rearrange("p (a b) -> p a b", b=32)
-        nc.vector.tensor_reduce(out=edge[:, 0:1], in_=id64[:, :, 0:2], axis=AX.XY, op=ALU.add)
-        nc.vector.tensor_reduce(out=edge[:, 1:2], in_=id64[:, :, 62:64], axis=AX.XY, op=ALU.add)
-        nc.vector.tensor_reduce(out=edge[:, 2:3], in_=id32[:, :, 0:2], axis=AX.XY, op=ALU.add)
-        nc.vector.tensor_reduce(out=edge[:, 3:4], in_=id32[:, :, 30:32], axis=AX.XY, op=ALU.add)
-        row_edge = keep.tile([P, 1], F32, name="row_edge")
-        col_edge = keep.tile([P, 1], F32, name="col_edge")
-        nc.vector.tensor_tensor(out=row_edge[:], in0=edge[:, 0:1], in1=edge[:, 1:2], op=ALU.add)
-        nc.vector.tensor_tensor(out=col_edge[:], in0=edge[:, 2:3], in1=edge[:, 3:4], op=ALU.add)
-        nc.vector.tensor_scalar(out=row_edge[:], in0=row_edge[:], scalar1=NEVER, scalar2=None, op0=ALU.mult)
-        nc.vector.tensor_scalar(out=col_edge[:], in0=col_edge[:], scalar1=NEVER, scalar2=None, op0=ALU.mult)
+                if c == 0:
+                    quantise(g_1b, c1, s1, NB)
+                if c + 1 < LC:
+                    g_0 = turn(raw_0[c + 1], "vs" if c % 2 == 0 else "ss")
+                for st in range(4, ST - 1):
+                    col_unit(st, c)
+                if c + 1 < LC:
+                    quantise(g_0, c0, s0, (c + 1) * NB)
+                col_unit(ST - 1, c)
 
         nmx = keep.tile([P, ST], F32, name="nmx")
         dd = keep.tile([P, ST * LC], F32, name="dd")
@@ -186,49 +208,64 @@ def tile_coarsematching_t_kernel(tc, feat_c0, feat_c1, temperature, out_0, out_1
             out=dd3, in0=nmx[:].unsqueeze(2).to_broadcast([P, ST, LC]), in1=nm_c3, op=ALU.subtract
         )
         nc.scalar.activation(out=dd[:], in_=dd[:], func=ACT.Exp)
+        row_front(0)
         nc.vector.tensor_tensor(out=dd[:], in0=dd[:], in1=sg_c[:], op=ALU.mult)
         nc.vector.tensor_reduce(out=tot[:], in_=dd3, axis=AX.X, op=ALU.add)
+        row_exp(0)
         nc.scalar.activation(out=tot[:], in_=tot[:], func=ACT.Ln)
+        row_front(1)
         nc.vector.tensor_tensor(out=b_col[:], in0=nmx[:], in1=tot[:], op=ALU.subtract)
-
-        for t in range(4):
-            row_unit(t)
-        row_norm(0, 4)
 
         with tc.tile_pool(name="main", bufs=1) as main:
             conf = main.tile([P, LT, S], F32, name="conf")
             best = main.tile([P, S], F32, name="best")
-            zero = main.tile([P, S], F32, name="zero")
-            nc.gpsimd.memset(zero[:], 0.0)
             nc.gpsimd.memset(best[:, 0:S_LO], 0.0)
             nc.gpsimd.memset(best[:, S_HI:S], 0.0)
-            nc.sync.dma_start(out=o1[0:P, :], in_=zero[:])
-            nc.sync.dma_start(out=o1[L - P : L, :], in_=zero[:])
-            for lo in (0, S_HI):
-                for first in (1, 16):
-                    nc.sync.dma_start(
-                        out=o1[first * P : (first + 15) * P, lo : lo + S_LO].rearrange("(j p) s -> p j s", p=P),
-                        in_=zero[:, 0 : 15 * S_LO].rearrange("p (j s) -> p j s", s=S_LO),
-                    )
+            w1s = {}
+            wbanks = {}
+            tbs = {}
 
-            def columns(c, w1, st):
+            def w_tile(c):
+                w1 = main.tile([P, ST, NB], F32, name="w1", tag="w1", bufs=2)
+                w1s[c] = w1
+
+            def w_mx(c, st):
                 bank = psm.tile([P, NB], F32, name="bank", tag="mx")
                 mx(bank[:], c1, s1, st * P, c0, s0, c * NB)
+                wbanks[(c, st)] = bank
+
+            def w_out(c, st):
                 nc.scalar.activation(
-                    out=w1[:, st, :], in_=bank[:], func=ACT.Identity, bias=b_col[:, st : st + 1], scale=t_two[:, 0:1]
+                    out=w1s[c][:, st, :],
+                    in_=wbanks[(c, st)][:],
+                    func=ACT.Identity,
+                    bias=b_col[:, st : st + 1],
+                    scale=t_two[:, 0:1],
                 )
 
-            def rows(c, w1, j):
-                t = 4 * c + j
+            def back(t):
+                w1 = w1s[t // 4]
+                j = t % 4
+                pair = []
                 for h in range(2):
                     tb = pst.tile([P, NB], F32, name="tb", tag="tr")
                     for q in range(4):
                         nc.tensor.transpose(
                             tb[:, q * P : (q + 1) * P], w1[:, 4 * h + q, j * P : (j + 1) * P], ident[:]
                         )
+                    pair.append(tb)
+                tbs[t] = pair
+
+            def e_exp(t):
+                for h in range(2):
                     nc.scalar.activation(
-                        out=conf[:, t, h * NB : (h + 1) * NB], in_=tb[:], func=ACT.Exp, bias=nm_r[:, t : t + 1]
+                        out=conf[:, t, h * NB : (h + 1) * NB],
+                        in_=tbs[t][h][:],
+                        func=ACT.Exp,
+                        bias=nm_r[:, t : t + 1],
                     )
+
+            def finish(t):
                 nc.vector.tensor_scalar(
                     out=conf[:, t, :],
                     in0=conf[:, t, :],
@@ -248,35 +285,51 @@ def tile_coarsematching_t_kernel(tc, feat_c0, feat_c1, temperature, out_0, out_1
                         out=best[:, S_LO:S_HI], in0=best[:, S_LO:S_HI], in1=conf[:, t, S_LO:S_HI], op=ALU.max
                     )
 
-            w1_now = main.tile([P, ST, NB], F32, name="w1", tag="w1", bufs=2)
+            w_tile(0)
             for st in range(ST):
-                columns(0, w1_now, st)
-            for c in range(LC):
-                w1_next = None
-                if c + 1 < LC:
-                    w1_next = main.tile([P, ST, NB], F32, name="w1", tag="w1", bufs=2)
-                for j in range(4):
-                    if c + 1 < LC:
-                        row_unit(4 * (c + 1) + j)
-                        columns(c + 1, w1_next, 2 * j)
-                        columns(c + 1, w1_next, 2 * j + 1)
-                    rows(c, w1_now, j)
-                if c + 1 < LC:
-                    row_norm(4 * (c + 1), 4)
-                w1_now = w1_next
-
-            rgate = main.tile([P, LT], F32, name="rgate")
-            nc.vector.tensor_scalar(out=rgate[:], in0=rmax[:], scalar1=THR, scalar2=NEVER, op0=ALU.is_le, op1=ALU.mult)
-            nc.vector.tensor_tensor(out=rgate[:], in0=rgate[:], in1=rmax[:], op=ALU.max)
-            nc.vector.tensor_scalar(out=rgate[:], in0=rgate[:], scalar1=row_edge[:, 0:1], scalar2=None, op0=ALU.max)
+                w_mx(0, st)
+                w_out(0, st)
+            w_tile(1)
+            for st in range(2):
+                w_mx(1, st)
+                w_out(1, st)
+            back(0)
+            for t in range(LT + 1):
+                k = t + 1
+                wc = 1 + k // 4
+                wst = 2 * (k % 4)
+                has_w = wc < LC
+                if has_w:
+                    if wst == 0:
+                        w_tile(wc)
+                    w_mx(wc, wst)
+                    w_mx(wc, wst + 1)
+                if t + 1 < LT:
+                    back(t + 1)
+                if t < LT:
+                    e_exp(t)
+                if has_w:
+                    w_out(wc, wst)
+                    w_out(wc, wst + 1)
+                if t + 1 < LT:
+                    row_exp(t + 1)
+                if t >= 1:
+                    finish(t - 1)
+                if t + 2 < LT:
+                    row_front(t + 2)
+                if t < LT:
+                    row_recip(t)
 
             cmax = main.tile([P, ST], F32, name="cmax")
+            tms = []
             for h in range(2):
                 tm = pst.tile([P, 4, P], F32, name="tm", tag="tr")
                 for q in range(4):
                     st = 4 * h + q
                     nc.tensor.transpose(tm[:, q, :], best[:, st * P : (st + 1) * P], ident[:])
-                nc.vector.tensor_reduce(out=cmax[:, 4 * h : 4 * h + 4], in_=tm[:], axis=AX.X, op=ALU.max)
+                tms.append(tm)
+            for h in range(2):
+                nc.vector.tensor_reduce(out=cmax[:, 4 * h : 4 * h + 4], in_=tms[h][:], axis=AX.X, op=ALU.max)
             nc.vector.tensor_scalar(out=cmax[:], in0=cmax[:], scalar1=col_edge[:, 0:1], scalar2=None, op0=ALU.max)
             spread = main.tile([P, ST, P], F32, name="spread")
             nc.vector.tensor_copy(out=spread[:], in_=cmax[:].unsqueeze(2).to_broadcast([P, ST, P]))
@@ -286,10 +339,14 @@ def tile_coarsematching_t_kernel(tc, feat_c0, feat_c1, temperature, out_0, out_1
                 for q in range(4):
                     nc.tensor.transpose(cb[:, q * P : (q + 1) * P], spread[:, 4 * h + q, :], ident[:])
                 cbs.append(cb)
+            rgate = main.tile([P, LT], F32, name="rgate")
+            nc.vector.tensor_scalar(out=rgate[:], in0=rmax[:], scalar1=THR, scalar2=NEVER, op0=ALU.is_le, op1=ALU.mult)
+            nc.vector.tensor_tensor(out=rgate[:], in0=rgate[:], in1=rmax[:], op=ALU.max)
+            nc.vector.tensor_scalar(out=rgate[:], in0=rgate[:], scalar1=row_edge[:, 0:1], scalar2=None, op0=ALU.max)
 
             half = S_IN // 2
             for t in range(1, LT - 1):
-                mask = main.tile([P, S_IN], BF16, name="mask", tag="mask", bufs=3)
+                mask = main.tile([P, S_IN], BF16, name="mask", tag="mask", bufs=2)
                 nc.vector.scalar_tensor_tensor(
                     out=mask[:, 0:half],
                     in0=cbs[0][:, S_LO:NB],
@@ -306,6 +363,6 @@ def tile_coarsematching_t_kernel(tc, feat_c0, feat_c1, temperature, out_0, out_1
                     op0=ALU.max,
                     op1=ALU.is_equal,
                 )
-                mc = main.tile([P, S_IN], F32, name="mc", tag="mc", bufs=N_MC)
+                mc = main.tile([P, S_IN], F32, name="mc", tag="mc", bufs=3)
                 nc.scalar.activation(out=mc[:], in_=mask[:], func=ACT.Copy, scale=rmax[:, t : t + 1])
                 nc.sync.dma_start(out=o1[t * P : (t + 1) * P, S_LO:S_HI], in_=mc[:])

import concourse.mybir as mybir
from concourse.masks import make_identity

F32 = mybir.dt.float32
BF16 = mybir.dt.bfloat16
U32 = mybir.dt.uint32
U8 = mybir.dt.uint8
FP8X4 = mybir.dt.float8_e4m3fn_x4
ALU = mybir.AluOpType
ACT = mybir.ActivationFunctionType
AX = mybir.AxisListType

P = 128
L = 4096
S = 1024
C = 512
LT = L // P
ST = S // P
NB = 512
LC = L // NB
THR = 0.2
INV_SQRT_C = 1.0 / float(C) ** 0.5
NEVER = 2.0
S_LO = 64
S_HI = 960
S_IN = S_HI - S_LO

FLOPS = 2 * L * S * C


def tile_coarsematching_t_kernel(tc, feat_c0, feat_c1, temperature, out_0, out_1):
    nc = tc.nc
    f0 = feat_c0.flatten_outer_dims()
    f1 = feat_c1.flatten_outer_dims()
    o0 = out_0.flatten_outer_dims()
    o1 = out_1.flatten_outer_dims()

    with tc.manual_schedule(), tc.tile_pool(name="keep", bufs=1) as keep, tc.tile_pool(
        name="junk", bufs=2
    ) as junk, tc.psum_pool(name="psm", bufs=4) as psm, tc.psum_pool(name="pst", bufs=4) as pst:
        ident = keep.tile([P, P], F32, name="ident")
        make_identity(nc, ident[:])

        t_bf = keep.tile([P, 1], BF16, name="t_bf")
        nc.sync.dma_start(out=t_bf[:], in_=temperature.partition_broadcast(P))

        c0 = keep.tile([P, L], U32, name="c0", align_bytes=64)
        s0 = keep.tile([P, L], U8, name="s0", align_bytes=64)
        c1 = keep.tile([P, S], U32, name="c1", align_bytes=64)
        s1 = keep.tile([P, S], U8, name="s1", align_bytes=64)

        nm_c = keep.tile([P, ST * LC], F32, name="nm_c")
        sg_c = keep.tile([P, ST * LC], F32, name="sg_c")
        nm_b = keep.tile([P, 2 * LT], F32, name="nm_b")
        nm_r = keep.tile([P, LT], F32, name="nm_r")
        rsum = keep.tile([P, LT], F32, name="rsum")
        r_inv = keep.tile([P, LT], F32, name="r_inv")
        rmax = keep.tile([P, LT], F32, name="rmax")
        t_pos = keep.tile([P, 1], F32, name="t_pos")
        t_neg = keep.tile([P, 1], F32, name="t_neg")
        t_two = keep.tile([P, 1], F32, name="t_two")
        edge = keep.tile([P, 4], F32, name="edge")
        row_edge = keep.tile([P, 1], F32, name="row_edge")
        col_edge = keep.tile([P, 1], F32, name="col_edge")

        def mx(bank, codes_a, scales_a, a_lo, codes_b, scales_b, b_lo):
            nc.tensor.matmul_mx(
                out=bank,
                lhsT=codes_a[:, a_lo : a_lo + P].bitcast(FP8X4),
                lhsT_scale=scales_a[:, a_lo : a_lo + P],
                rhs=codes_b[:, b_lo : b_lo + NB].bitcast(FP8X4),
                rhs_scale=scales_b[:, b_lo : b_lo + NB],
                start=True,
                stop=True,
            )

        def neg_max(dst, bank, nm_col):
            nc.vector.tensor_scalar(
                out=dst, in0=bank, scalar1=t_neg[:, 0:1], scalar2=None, op0=ALU.mult, op1=ALU.min, accum_out=nm_col
            )

        def col_unit(st, c):
            col = LC * st + c
            bank = psm.tile([P, NB], F32, name="bank", tag="mx")
            mx(bank[:], c1, s1, st * P, c0, s0, c * NB)
            jv = junk.tile([P, NB], BF16, name="jv", tag="jv")
            neg_max(jv[:], bank[:], nm_c[:, col : col + 1])
            js = junk.tile([P, NB], BF16, name="js", tag="js")
            nc.scalar.activation(
                out=js[:],
                in_=bank[:],
                func=ACT.Exp,
                bias=nm_c[:, col : col + 1],
                scale=t_pos[:, 0:1],
                accum_out=sg_c[:, col : col + 1],
            )

        nxs = {}

        def row_front(t):
            nx = junk.tile([P, S], F32, name="nx", tag="nx", bufs=3)
            for h in range(2):
                bank = psm.tile([P, NB], F32, name="bank", tag="mx")
                mx(bank[:], c0, s0, t * P, c1, s1, h * NB)
                neg_max(nx[:, h * NB : (h + 1) * NB], bank[:], nm_b[:, 2 * t + h : 2 * t + h + 1])
            nc.vector.tensor_tensor(
                out=nm_r[:, t : t + 1], in0=nm_b[:, 2 * t : 2 * t + 1], in1=nm_b[:, 2 * t + 1 : 2 * t + 2], op=ALU.min
            )
            nxs[t] = nx

        def row_exp(t):
            nx = nxs[t]
            nc.scalar.activation(
                out=nx[:], in_=nx[:], func=ACT.Exp, bias=nm_r[:, t : t + 1], scale=-1.0, accum_out=rsum[:, t : t + 1]
            )

        def row_recip(t):
            nc.vector.reciprocal(out=r_inv[:, t : t + 1], in_=rsum[:, t : t + 1])

        with tc.tile_pool(name="head", bufs=3) as head:
            zero = head.tile([P, S], F32, name="zero", bufs=1)
            nc.gpsimd.memset(zero[:], 0.0)

            def load(src_rows, name):
                raw = head.tile([P, 4, C], BF16, name=name, bufs=1)
                nc.sync.dma_start(out=raw[:], in_=src_rows.rearrange("(t p) k -> p t k", p=P))
                return raw

            raw_1a = load(f1[0:NB, :], "raw_1a")
            raw_0 = [load(f0[0:NB, :], "raw_00")]
            raw_1b = load(f1[NB:S, :], "raw_1b")
            for c in range(1, LC):
                raw_0.append(load(f0[c * NB : (c + 1) * NB, :], "raw_0%d" % c))
            nc.sync.dma_start(out=o1[0:P, :], in_=zero[:])
            nc.sync.dma_start(out=o1[L - P : L, :], in_=zero[:])
            for lo in (0, S_HI):
                for first in (1, 16):
                    nc.sync.dma_start(
                        out=o1[first * P : (first + 15) * P, lo : lo + S_LO].rearrange("(j p) s -> p j s", p=P),
                        in_=zero[:, 0 : 15 * S_LO].rearrange("p (j s) -> p j s", s=S_LO),
                    )

            nc.vector.tensor_copy(out=t_pos[:], in_=t_bf[:])
            nc.vector.tensor_scalar(out=t_neg[:], in0=t_bf[:], scalar1=-1.0, scalar2=None, op0=ALU.mult)
            nc.vector.tensor_scalar(out=t_two[:], in0=t_bf[:], scalar1=2.0, scalar2=None, op0=ALU.mult)
            id64 = ident[:].rearrange("p (a b) -> p a b", b=64)
            id32 = ident[:].rearrange("p (a b) -> p a b", b=32)
            nc.vector.tensor_reduce(out=edge[:, 0:1], in_=id64[:, :, 0:2], axis=AX.XY, op=ALU.add)
            nc.vector.tensor_reduce(out=edge[:, 1:2], in_=id64[:, :, 62:64], axis=AX.XY, op=ALU.add)
            nc.vector.tensor_reduce(out=edge[:, 2:3], in_=id32[:, :, 0:2], axis=AX.XY, op=ALU.add)
            nc.vector.tensor_reduce(out=edge[:, 3:4], in_=id32[:, :, 30:32], axis=AX.XY, op=ALU.add)
            nc.vector.tensor_tensor(out=row_edge[:], in0=edge[:, 0:1], in1=edge[:, 1:2], op=ALU.add)
            nc.vector.tensor_tensor(out=col_edge[:], in0=edge[:, 2:3], in1=edge[:, 3:4], op=ALU.add)
            nc.vector.tensor_scalar(out=row_edge[:], in0=row_edge[:], scalar1=NEVER, scalar2=None, op0=ALU.mult)
            nc.vector.tensor_scalar(out=col_edge[:], in0=col_edge[:], scalar1=NEVER, scalar2=None, op0=ALU.mult)

            def turn(raw, engines):
                grouped = head.tile([P, NB, 4], BF16, name="grouped", tag="grouped", align_bytes=64)
                for half in range(2):
                    bank = pst.tile([P, 2, 256], F32, name="tbank", tag="tr")
                    for i in range(2):
                        words = raw[:, 2 * half + i, :].bitcast(F32)
                        for u in range(2):
                            nc.tensor.transpose(
                                bank[:, u, P * i : P * (i + 1)], words[:, P * u : P * (u + 1)], ident[:]
                            )
                    src = bank[:].bitcast(BF16).rearrange("p u (l e) -> p l u e", e=2)
                    dst = grouped[:, 256 * half : 256 * (half + 1), :].rearrange("p l (u e) -> p l u e", e=2)
                    if engines[half] == "v":
                        nc.vector.tensor_scalar(out=dst, in0=src, scalar1=INV_SQRT_C, scalar2=None, op0=ALU.mult)
                    else:
                        nc.scalar.activation(out=dst, in_=src, func=ACT.Copy, scale=INV_SQRT_C)
                return grouped

            def quantise(grouped, codes, scales, lo):
                nc.vector.quantize_mx(
                    out=codes[:, lo : lo + NB].bitcast(FP8X4),
                    scales=scales[:, lo : lo + NB],
                    in_=grouped[:].rearrange("p l j -> p (l j)"),
                )

            g_1a = turn(raw_1a, "vs")
            g_0 = turn(raw_0[0], "vs")
            quantise(g_1a, c1, s1, 0)
            g_1b = turn(raw_1b, "vs")
            quantise(g_0, c0, s0, 0)
            for c in range(LC):
                for st in range(4):
                    col_unit(st, c)
                if c == 0:
                    quantise(g_1b, c1, s1, NB)
                if c + 1 < LC:
                    g_0 = turn(raw_0[c + 1], "vs" if c % 2 == 0 else "ss")
                for st in range(4, ST - 1):
                    col_unit(st, c)
                if c + 1 < LC:
                    quantise(g_0, c0, s0, (c + 1) * NB)
                col_unit(ST - 1, c)

        nmx = keep.tile([P, ST], F32, name="nmx")
        dd = keep.tile([P, ST * LC], F32, name="dd")
        tot = keep.tile([P, ST], F32, name="tot")
        b_col = keep.tile([P, ST], F32, name="b_col")
        nm_c3 = nm_c[:].rearrange("p (s c) -> p s c", c=LC)
        dd3 = dd[:].rearrange("p (s c) -> p s c", c=LC)
        nc.vector.tensor_reduce(out=nmx[:], in_=nm_c3, axis=AX.X, op=ALU.min)
        nc.vector.tensor_tensor(
            out=dd3, in0=nmx[:].unsqueeze(2).to_broadcast([P, ST, LC]), in1=nm_c3, op=ALU.subtract
        )
        nc.scalar.activation(out=dd[:], in_=dd[:], func=ACT.Exp)
        row_front(0)
        nc.vector.tensor_tensor(out=dd[:], in0=dd[:], in1=sg_c[:], op=ALU.mult)
        nc.vector.tensor_reduce(out=tot[:], in_=dd3, axis=AX.X, op=ALU.add)
        row_exp(0)
        nc.scalar.activation(out=tot[:], in_=tot[:], func=ACT.Ln)
        row_front(1)
        nc.vector.tensor_tensor(out=b_col[:], in0=nmx[:], in1=tot[:], op=ALU.subtract)

        with tc.tile_pool(name="main", bufs=1) as main:
            conf = main.tile([P, LT, S], F32, name="conf")
            best = main.tile([P, S], F32, name="best")
            nc.gpsimd.memset(best[:, 0:S_LO], 0.0)
            nc.gpsimd.memset(best[:, S_HI:S], 0.0)
            w1s = {}
            wbanks = {}
            tbs = {}

            def w_tile(c):
                w1 = main.tile([P, ST, NB], F32, name="w1", tag="w1", bufs=2)
                w1s[c] = w1

            def w_mx(c, st):
                bank = psm.tile([P, NB], F32, name="bank", tag="mx")
                mx(bank[:], c1, s1, st * P, c0, s0, c * NB)
                wbanks[(c, st)] = bank

            def w_out(c, st):
                nc.scalar.activation(
                    out=w1s[c][:, st, :],
                    in_=wbanks[(c, st)][:],
                    func=ACT.Identity,
                    bias=b_col[:, st : st + 1],
                    scale=t_two[:, 0:1],
                )

            def back(t):
                w1 = w1s[t // 4]
                j = t % 4
                pair = []
                for h in range(2):
                    tb = pst.tile([P, NB], F32, name="tb", tag="tr")
                    for q in range(4):
                        nc.tensor.transpose(
                            tb[:, q * P : (q + 1) * P], w1[:, 4 * h + q, j * P : (j + 1) * P], ident[:]
                        )
                    pair.append(tb)
                tbs[t] = pair

            def e_exp(t):
                for h in range(2):
                    nc.scalar.activation(
                        out=conf[:, t, h * NB : (h + 1) * NB],
                        in_=tbs[t][h][:],
                        func=ACT.Exp,
                        bias=nm_r[:, t : t + 1],
                    )

            def finish(t):
                nc.vector.tensor_scalar(
                    out=conf[:, t, :],
                    in0=conf[:, t, :],
                    scalar1=r_inv[:, t : t + 1],
                    scalar2=None,
                    op0=ALU.mult,
                    op1=ALU.max,
                    accum_out=rmax[:, t : t + 1],
                )
                nc.sync.dma_start(out=o0[t * P : (t + 1) * P, :], in_=conf[:, t, :])
                if t == 1:
                    nc.vector.tensor_tensor(
                        out=best[:, S_LO:S_HI], in0=conf[:, 0, S_LO:S_HI], in1=conf[:, 1, S_LO:S_HI], op=ALU.max
                    )
                elif t > 1:
                    nc.vector.tensor_tensor(
                        out=best[:, S_LO:S_HI], in0=best[:, S_LO:S_HI], in1=conf[:, t, S_LO:S_HI], op=ALU.max
                    )

            w_tile(0)
            for st in range(ST):
                w_mx(0, st)
                w_out(0, st)
            w_tile(1)
            for st in range(2):
                w_mx(1, st)
                w_out(1, st)
            back(0)
            for t in range(LT + 1):
                k = t + 1
                wc = 1 + k // 4
                wst = 2 * (k % 4)
                has_w = wc < LC
                if has_w:
                    if wst == 0:
                        w_tile(wc)
                    w_mx(wc, wst)
                    w_mx(wc, wst + 1)
                if t + 1 < LT:
                    back(t + 1)
                if t < LT:
                    e_exp(t)
                if has_w:
                    w_out(wc, wst)
                    w_out(wc, wst + 1)
                if t + 1 < LT:
                    row_exp(t + 1)
                if t >= 1:
                    finish(t - 1)
                if t + 2 < LT:
                    row_front(t + 2)
                if t < LT:
                    row_recip(t)

            cmax = main.tile([P, ST], F32, name="cmax")
            tms = []
            for h in range(2):
                tm = pst.tile([P, 4, P], F32, name="tm", tag="tr")
                for q in range(4):
                    st = 4 * h + q
                    nc.tensor.transpose(tm[:, q, :], best[:, st * P : (st + 1) * P], ident[:])
                tms.append(tm)
            for h in range(2):
                nc.vector.tensor_reduce(out=cmax[:, 4 * h : 4 * h + 4], in_=tms[h][:], axis=AX.X, op=ALU.max)
            nc.vector.tensor_scalar(out=cmax[:], in0=cmax[:], scalar1=col_edge[:, 0:1], scalar2=None, op0=ALU.max)
            spread = main.tile([P, ST, P], F32, name="spread")
            nc.vector.tensor_copy(out=spread[:], in_=cmax[:].unsqueeze(2).to_broadcast([P, ST, P]))
            cbs = []
            for h in range(2):
                cb = pst.tile([P, NB], F32, name="cb", tag="tr")
                for q in range(4):
                    nc.tensor.transpose(cb[:, q * P : (q + 1) * P], spread[:, 4 * h + q, :], ident[:])
                cbs.append(cb)
            rgate = main.tile([P, LT], F32, name="rgate")
            nc.vector.tensor_scalar(out=rgate[:], in0=rmax[:], scalar1=THR, scalar2=NEVER, op0=ALU.is_le, op1=ALU.mult)
            nc.vector.tensor_tensor(out=rgate[:], in0=rgate[:], in1=rmax[:], op=ALU.max)
            nc.vector.tensor_scalar(out=rgate[:], in0=rgate[:], scalar1=row_edge[:, 0:1], scalar2=None, op0=ALU.max)

            half = S_IN // 2
            for t in range(1, LT - 1):
                mask = main.tile([P, S_IN], BF16, name="mask", tag="mask", bufs=2)
                nc.vector.scalar_tensor_tensor(
                    out=mask[:, 0:half],
                    in0=cbs[0][:, S_LO:NB],
                    scalar=rgate[:, t : t + 1],
                    in1=conf[:, t, S_LO:NB],
                    op0=ALU.max,
                    op1=ALU.is_equal,
                )
                nc.vector.scalar_tensor_tensor(
                    out=mask[:, half:S_IN],
                    in0=cbs[1][:, 0 : S_HI - NB],
                    scalar=rgate[:, t : t + 1],
                    in1=conf[:, t, NB:S_HI],
                    op0=ALU.max,
                    op1=ALU.is_equal,
                )
                mc = main.tile([P, S_IN], F32, name="mc", tag="mc", bufs=3)
                nc.scalar.activation(out=mc[:], in_=mask[:], func=ACT.Copy, scale=rmax[:, t : t + 1])
                nc.sync.dma_start(out=o1[t * P : (t + 1) * P, S_LO:S_HI], in_=mc[:])
